import numpy as np
import ml_dtypes


def mxq(x, axis, fmt="e4m3"):
    dtype, down = {"e4m3": (ml_dtypes.float8_e4m3fn, 7), "e5m2": (ml_dtypes.float8_e5m2, 14)}[fmt]
    v = np.moveaxis(np.asarray(x, np.float32).astype(ml_dtypes.bfloat16).astype(np.float64), axis, -1)
    blocks = v.reshape(v.shape[:-1] + (-1, 32))
    amax = np.abs(blocks).max(-1, keepdims=True)
    byte = np.maximum(np.where(amax > 0, np.frexp(amax)[1] - 1 + 127, 0) - down, 1)
    scale = np.exp2(byte - 127.0)
    codes = (blocks / scale).astype(np.float32).astype(dtype).astype(np.float64)
    return np.moveaxis((codes * scale).reshape(v.shape), -1, axis)


WIDE = False


def mx_kscale(k):
    if not WIDE:
        return np.ones(k)
    levels = np.array([10, -10, 5, -5, 0])
    a = np.random.permutation(np.resize(levels, k // 512 * 4)).reshape(k // 512, 4)
    idx = np.arange(k)
    return np.exp2(a[idx // 512, idx % 128 // 32])


BF16 = ml_dtypes.bfloat16


def bf(x):
    return np.asarray(x, np.float32).astype(BF16)


def f64(x):
    return np.asarray(x).astype(np.float64)


G, NSPIN, D_ONE, D_TWO = 128, 8, 512, 256
N = 2 * G * NSPIN
K1 = D_ONE + 2 * D_TWO
K2 = 2 * D_ONE
TANH_GAIN = 1.5927812698663606


def setup_inputs():
    s = mx_kscale(K1)[D_ONE:]
    w1 = np.random.standard_normal((K1, D_ONE)) / np.sqrt(K1)
    w1[D_ONE:] = w1[D_ONE:] / s[:, None]
    return {"h_one": bf(np.random.standard_normal((N, D_ONE))),
            "h_two_same": bf(np.random.standard_normal((N * NSPIN, D_TWO)) * 2.0 * s[:D_TWO]),
            "h_two_diff": bf(np.random.standard_normal((N * NSPIN, D_TWO)) * 2.0 * s[D_TWO:]),
            "W1": bf(w1),
            "b1": bf(np.random.standard_normal(D_ONE) * 0.3),
            "Wg": bf(np.random.standard_normal((K2, D_ONE)) * 2.0 / np.sqrt(K2))}


def reference(h_one, h_two_same, h_two_diff, W1, b1, Wg):
    h = f64(h_one)
    sqrt2 = np.sqrt(2.0)
    g_mean = h.reshape(G, 2, NSPIN, D_ONE).mean(axis=2)
    g_inp = np.stack([
        np.concatenate([g_mean[:, 0], g_mean[:, 1]], axis=-1),
        np.concatenate([g_mean[:, 1], g_mean[:, 0]], axis=-1),
    ], axis=1).reshape(2 * G, K2)
    pair_same = f64(h_two_same).reshape(N, NSPIN, D_TWO).mean(axis=1)
    pair_diff = f64(h_two_diff).reshape(N, NSPIN, D_TWO).mean(axis=1)
    one_in = np.concatenate([h, pair_same, pair_diff], axis=-1)
    h_new = (mxq(one_in, 1, "e4m3") @ mxq(f64(W1), 0, "e4m3")) + f64(b1)
    global_new = mxq(g_inp, 1, "e4m3") @ mxq(f64(Wg), 0, "e4m3")
    global_new = np.repeat(global_new, NSPIN, axis=0)
    h_new = TANH_GAIN * np.tanh((h_new + global_new) / sqrt2)
    return (h + h_new) / sqrt2

@@ -1,0 +1,253 @@
+from contextlib import ExitStack
+import math
+
+import concourse.mybir as mybir
+from concourse.masks import make_identity
+
+F32 = mybir.dt.float32
+BF16 = mybir.dt.bfloat16
+U32 = mybir.dt.uint32
+U8 = mybir.dt.uint8
+FP8X4 = mybir.dt.float8_e4m3fn_x4
+ADD = mybir.AluOpType.add
+MULT = mybir.AluOpType.mult
+
+P = 128
+PACK = 4
+NSPIN = 8
+D_ONE = 512
+D_TWO = 256
+ELECTRONS = 2048
+TILES = ELECTRONS // P
+CHUNK_TILES = 4
+CHUNK = CHUNK_TILES * P
+TILE_GROUPS = P // NSPIN
+CHUNK_GROUPS = CHUNK // NSPIN
+UNIT_ROWS = P * NSPIN
+UNIT_BUFS = 20
+
+TANH_GAIN = 1.5927812698663606
+INV_SQRT2 = 1.0 / math.sqrt(2.0)
+
+FLOPS = 2 * (ELECTRONS + ELECTRONS // NSPIN) * 1024 * D_ONE
+
+
+def tile_fermilayer_pa_kernel(tc, h_one, h_two_same, h_two_diff, W1, b1, Wg, out):
+    nc = tc.nc
+    with ExitStack() as ctx:
+        const = ctx.enter_context(tc.tile_pool(name="const", bufs=1))
+        w_stage = ctx.enter_context(tc.tile_pool(name="w_stage", bufs=2))
+        h_pool = ctx.enter_context(tc.tile_pool(name="h_pool", bufs=TILES // CHUNK_TILES))
+        chunk_pool = ctx.enter_context(tc.tile_pool(name="chunk_pool", bufs=2))
+        units = ctx.enter_context(tc.tile_pool(name="units", bufs=UNIT_BUFS))
+        sums = ctx.enter_context(tc.tile_pool(name="sums", bufs=2))
+        tile_pool = ctx.enter_context(tc.tile_pool(name="tile_pool", bufs=3))
+        out_pool = ctx.enter_context(tc.tile_pool(name="out_pool", bufs=8))
+        psum_t = ctx.enter_context(tc.psum_pool(name="psum_t", bufs=2))
+        psum_g = ctx.enter_context(tc.psum_pool(name="psum_g", bufs=1))
+        psum_pair = ctx.enter_context(tc.psum_pool(name="psum_pair", bufs=2))
+        psum_acc = ctx.enter_context(tc.psum_pool(name="psum_acc", bufs=3))
+
+        ident_bf = const.tile([P, P], BF16, name="ident_bf")
+        make_identity(nc, ident_bf[:])
+        ident_f32 = const.tile([P, P], F32, name="ident_f32")
+        make_identity(nc, ident_f32[:])
+        pool_f32 = const.tile([P, TILE_GROUPS], F32, name="pool_f32")
+        nc.vector.tensor_reduce(
+            out=pool_f32[:],
+            in_=ident_f32[:].rearrange("p (c i) -> p c i", i=NSPIN),
+            axis=mybir.AxisListType.X,
+            op=ADD,
+        )
+        pool_rows = const.tile([P, TILE_GROUPS], BF16, name="pool_rows")
+        nc.vector.tensor_copy(out=pool_rows[:], in_=pool_f32[:])
+
+        b_rows = const.tile([P, P], BF16, name="b_rows")
+        nc.vector.memset(b_rows[:], 0.0)
+        nc.scalar.dma_start(out=b_rows[0:PACK, :], in_=b1.rearrange("(r c) -> r c", c=P))
+        b_cols_ps = psum_t.tile([P, P], BF16, name="b_cols_ps", tag="hT")
+        nc.tensor.transpose(b_cols_ps[:], b_rows[:], ident_bf[:])
+        b_cols = const.tile([P, PACK, P], F32, name="b_cols")
+        nc.vector.tensor_copy(
+            out=b_cols[:], in_=b_cols_ps[:, 0:PACK].unsqueeze(2).to_broadcast([P, PACK, P])
+        )
+        b_rep_ps = psum_acc.tile([P, D_ONE], F32, name="b_rep_ps", tag="acc")
+        for r in range(PACK):
+            nc.tensor.transpose(b_rep_ps[:, P * r : P * (r + 1)], b_cols[:, r, :], ident_f32[:])
+        b1_rep = const.tile([P, D_ONE], F32, name="b1_rep")
+        nc.vector.tensor_copy(out=b1_rep[:], in_=b_rep_ps[:])
+
+        w_codes = const.tile([P, 4, D_ONE], U32, name="w_codes", align_bytes=64)
+        w_scales = const.tile([P, 4, D_ONE], U8, name="w_scales", align_bytes=64)
+        for w_index, w_dram in enumerate((W1, Wg)):
+            w_raw = w_stage.tile([P, 2 * PACK, D_ONE], BF16, name="w_raw")
+            nc.sync.dma_start(out=w_raw[:], in_=w_dram.rearrange("(c p) f -> p c f", p=P))
+            grouped = []
+            for half in range(2):
+                w_grouped = w_stage.tile([P, D_ONE, PACK], BF16, name="w_grouped", align_bytes=64)
+                nc.vector.tensor_copy(
+                    out=w_grouped[:],
+                    in_=w_raw[:, PACK * half : PACK * (half + 1), :].rearrange("p t f -> p f t"),
+                )
+                grouped.append(w_grouped)
+            for half in range(2):
+                nc.vector.quantize_mx(
+                    out=w_codes[:, 2 * w_index + half, :].bitcast(FP8X4),
+                    scales=w_scales[:, 2 * w_index + half, :],
+                    in_=grouped[half][:].rearrange("p f t -> p (f t)"),
+                )
+
+        def prepare_chunk(q):
+            h_nat = h_pool.tile([P, CHUNK_TILES, D_ONE], BF16, name="h_nat")
+            nc.sync.dma_start(
+                out=h_nat[:],
+                in_=h_one[CHUNK * q : CHUNK * (q + 1), :].rearrange("(n p) f -> p n f", p=P),
+            )
+            x_codes = chunk_pool.tile([P, 3, CHUNK], U32, name="x_codes", align_bytes=64)
+            x_scales = chunk_pool.tile([P, 3, CHUNK], U8, name="x_scales", align_bytes=64)
+            h_grouped = chunk_pool.tile([P, CHUNK, PACK], BF16, name="h_grouped", align_bytes=64)
+            g_sum = psum_g.tile([P, PACK, CHUNK_GROUPS], F32, name="g_sum")
+            for n in range(CHUNK_TILES):
+                hT = psum_t.tile([P, PACK, P], BF16, name="hT", tag="hT")
+                for t in range(PACK):
+                    nc.tensor.transpose(hT[:, t, :], h_nat[:, n, P * t : P * (t + 1)], ident_bf[:])
+                nc.scalar.copy(
+                    out=h_grouped[:, P * n : P * (n + 1), :], in_=hT[:].rearrange("p t e -> p e t")
+                )
+                for t in range(PACK):
+                    nc.tensor.matmul(
+                        out=g_sum[:, t, TILE_GROUPS * n : TILE_GROUPS * (n + 1)],
+                        lhsT=h_nat[:, n, P * t : P * (t + 1)],
+                        rhs=pool_rows[:],
+                        start=True,
+                        stop=True,
+                    )
+            g_means = chunk_pool.tile([P, 2, CHUNK_GROUPS, PACK], BF16, name="g_means")
+            nc.scalar.mul(
+                out=g_means[:, 0, :, :], in_=g_sum[:].rearrange("p t g -> p g t"), mul=1.0 / NSPIN
+            )
+            partner = g_means[:, 1, :, :].rearrange("p (m s) t -> p m s t", s=2)
+            by_spin = g_sum[:].rearrange("p t (m s) -> p m s t", s=2)
+            for s in range(2):
+                nc.scalar.mul(out=partner[:, :, 1 - s, :], in_=by_spin[:, :, s, :], mul=1.0 / NSPIN)
+            repeated = []
+            for c in range(2):
+                g_rep = chunk_pool.tile(
+                    [P, CHUNK_GROUPS, NSPIN, PACK], BF16, name="g_rep", align_bytes=64
+                )
+                nc.vector.tensor_copy(
+                    out=g_rep[:],
+                    in_=g_means[:, c, :, :]
+                    .unsqueeze(2)
+                    .to_broadcast([P, CHUNK_GROUPS, NSPIN, PACK]),
+                )
+                repeated.append(g_rep)
+            nc.vector.quantize_mx(
+                out=x_codes[:, 0, :].bitcast(FP8X4),
+                scales=x_scales[:, 0, :],
+                in_=h_grouped[:].rearrange("p e t -> p (e t)"),
+            )
+            for c in range(2):
+                nc.vector.quantize_mx(
+                    out=x_codes[:, 1 + c, :].bitcast(FP8X4),
+                    scales=x_scales[:, 1 + c, :],
+                    in_=repeated[c][:].rearrange("p g i t -> p (g i t)"),
+                )
+            return h_nat, x_codes, x_scales
+
+        def sum_rows_on_tensor_engine(stream, te, pooled_half):
+            rows = units.tile([P, NSPIN, D_TWO], BF16, name="rows", tag="unit")
+            nc.sync.dma_start(
+                out=rows[:],
+                in_=stream[UNIT_ROWS * te : UNIT_ROWS * (te + 1), :].rearrange(
+                    "(r p) f -> p r f", p=P
+                ),
+            )
+            for r in range(NSPIN):
+                for fh in range(2):
+                    nc.tensor.matmul(
+                        out=pooled_half[:, fh, TILE_GROUPS * r : TILE_GROUPS * (r + 1)],
+                        lhsT=rows[:, r, P * fh : P * (fh + 1)],
+                        rhs=pool_rows[:],
+                        start=True,
+                        stop=True,
+                    )
+
+        def sum_rows_by_adds(stream, te, pooled_half):
+            rows = units.tile([P, NSPIN, D_TWO], BF16, name="rows", tag="unit")
+            nc.sync.dma_start(
+                out=rows[:],
+                in_=stream[UNIT_ROWS * te : UNIT_ROWS * (te + 1), :].rearrange(
+                    "(p j) f -> p j f", j=NSPIN
+                ),
+            )
+            sum4 = sums.tile([P, 4, D_TWO], F32, name="sum4")
+            nc.vector.tensor_tensor(out=sum4[:], in0=rows[:, 0:4, :], in1=rows[:, 4:8, :], op=ADD)
+            sum2 = sums.tile([P, 2, D_TWO], F32, name="sum2")
+            nc.vector.tensor_tensor(out=sum2[:], in0=sum4[:, 0:2, :], in1=sum4[:, 2:4, :], op=ADD)
+            sum1 = sums.tile([P, D_TWO], F32, name="sum1")
+            nc.vector.tensor_tensor(out=sum1[:], in0=sum2[:, 0, :], in1=sum2[:, 1, :], op=ADD)
+            for fh in range(2):
+                nc.tensor.transpose(
+                    pooled_half[:, fh, :], sum1[:, P * fh : P * (fh + 1)], ident_f32[:]
+                )
+
+        for te in range(TILES):
+            n = te % CHUNK_TILES
+            if n == 0:
+                h_nat, x_codes, x_scales = prepare_chunk(te // CHUNK_TILES)
+            cols = slice(P * n, P * (n + 1))
+
+            pooled = psum_pair.tile([P, PACK, P], F32, name="pooled")
+            if te % 2 == 0:
+                sum_rows_by_adds(h_two_diff, te, pooled[:, 2:4, :])
+            else:
+                sum_rows_on_tensor_engine(h_two_diff, te, pooled[:, 2:4, :])
+            sum_rows_on_tensor_engine(h_two_same, te, pooled[:, 0:2, :])
+
+            pair_grouped = tile_pool.tile([P, P, PACK], BF16, name="pair_grouped", align_bytes=64)
+            nc.scalar.mul(
+                out=pair_grouped[:], in_=pooled[:].rearrange("p t e -> p e t"), mul=1.0 / NSPIN
+            )
+            pair_codes = tile_pool.tile([P, P], U32, name="pair_codes", align_bytes=64)
+            pair_scales = tile_pool.tile([P, P], U8, name="pair_scales", align_bytes=64)
+            nc.vector.quantize_mx(
+                out=pair_codes[:].bitcast(FP8X4),
+                scales=pair_scales[:],
+                in_=pair_grouped[:].rearrange("p e t -> p (e t)"),
+            )
+
+            acc = psum_acc.tile([P, D_ONE], F32, name="acc", tag="acc")
+            passes = (
+                (x_codes[:, 0, cols], x_scales[:, 0, cols], 0),
+                (x_codes[:, 1, cols], x_scales[:, 1, cols], 2),
+                (x_codes[:, 2, cols], x_scales[:, 2, cols], 3),
+                (pair_codes[:], pair_scales[:], 1),
+            )
+            for i, (codes, scales, w) in enumerate(passes):
+                nc.tensor.matmul_mx(
+                    out=acc[:],
+                    lhsT=codes.bitcast(FP8X4),
+                    lhsT_scale=scales,
+                    rhs=w_codes[:, w, :].bitcast(FP8X4),
+                    rhs_scale=w_scales[:, w, :],
+                    start=(i == 0),
+                    stop=(i == len(passes) - 1),
+                )
+
+            z = tile_pool.tile([P, D_ONE], F32, name="z")
+            nc.vector.tensor_tensor(out=z[:], in0=acc[:], in1=b1_rep[:], op=ADD)
+            nc.scalar.activation(
+                out=z[:], in_=z[:], func=mybir.ActivationFunctionType.Tanh, scale=INV_SQRT2
+            )
+            result = out_pool.tile([P, D_ONE], F32, name="result")
+            nc.scalar.mul(out=result[:], in_=h_nat[:, n, :], mul=INV_SQRT2)
+            nc.vector.scalar_tensor_tensor(
+                out=result[:],
+                in0=z[:],
+                scalar=TANH_GAIN * INV_SQRT2,
+                in1=result[:],
+                op0=MULT,
+                op1=ADD,
+            )
+            nc.sync.dma_start(out=out[P * te : P * (te + 1), :], in_=result[:])

@@ -48,6 +48,10 @@ def tile_fermilayer_pa_kernel(tc, h_one, h_two_same, h_two_diff, W1, b1, Wg, out
         psum_pair = ctx.enter_context(tc.psum_pool(name="psum_pair", bufs=2))
         psum_acc = ctx.enter_context(tc.psum_pool(name="psum_acc", bufs=3))
 
+        b_row = const.tile([P, D_ONE], BF16, name="b_row")
+        nc.vector.memset(b_row[:], 0.0)
+        nc.sync.dma_start(out=b_row[0:1, :], in_=b1.rearrange("(r c) -> r c", r=1))
+
         ident_bf = const.tile([P, P], BF16, name="ident_bf")
         make_identity(nc, ident_bf[:])
         ident_f32 = const.tile([P, P], F32, name="ident_f32")
@@ -62,18 +66,10 @@ def tile_fermilayer_pa_kernel(tc, h_one, h_two_same, h_two_diff, W1, b1, Wg, out
         pool_rows = const.tile([P, TILE_GROUPS], BF16, name="pool_rows")
         nc.vector.tensor_copy(out=pool_rows[:], in_=pool_f32[:])
 
-        b_rows = const.tile([P, P], BF16, name="b_rows")
-        nc.vector.memset(b_rows[:], 0.0)
-        nc.scalar.dma_start(out=b_rows[0:PACK, :], in_=b1.rearrange("(r c) -> r c", c=P))
-        b_cols_ps = psum_t.tile([P, P], BF16, name="b_cols_ps", tag="hT")
-        nc.tensor.transpose(b_cols_ps[:], b_rows[:], ident_bf[:])
-        b_cols = const.tile([P, PACK, P], F32, name="b_cols")
-        nc.vector.tensor_copy(
-            out=b_cols[:], in_=b_cols_ps[:, 0:PACK].unsqueeze(2).to_broadcast([P, PACK, P])
-        )
+        ones = const.tile([P, P], BF16, name="ones")
+        nc.vector.memset(ones[:], 1.0)
         b_rep_ps = psum_acc.tile([P, D_ONE], F32, name="b_rep_ps", tag="acc")
-        for r in range(PACK):
-            nc.tensor.transpose(b_rep_ps[:, P * r : P * (r + 1)], b_cols[:, r, :], ident_f32[:])
+        nc.tensor.matmul(out=b_rep_ps[:], lhsT=ones[:], rhs=b_row[:], start=True, stop=True)
         b1_rep = const.tile([P, D_ONE], F32, name="b1_rep")
         nc.vector.tensor_copy(out=b1_rep[:], in_=b_rep_ps[:])
 
@@ -183,14 +179,16 @@ def tile_fermilayer_pa_kernel(tc, h_one, h_two_same, h_two_diff, W1, b1, Wg, out
             )
             sum4 = sums.tile([P, 4, D_TWO], F32, name="sum4")
             nc.vector.tensor_tensor(out=sum4[:], in0=rows[:, 0:4, :], in1=rows[:, 4:8, :], op=ADD)
-            sum2 = sums.tile([P, 2, D_TWO], F32, name="sum2")
-            nc.vector.tensor_tensor(out=sum2[:], in0=sum4[:, 0:2, :], in1=sum4[:, 2:4, :], op=ADD)
-            sum1 = sums.tile([P, D_TWO], F32, name="sum1")
-            nc.vector.tensor_tensor(out=sum1[:], in0=sum2[:, 0, :], in1=sum2[:, 1, :], op=ADD)
             for fh in range(2):
-                nc.tensor.transpose(
-                    pooled_half[:, fh, :], sum1[:, P * fh : P * (fh + 1)], ident_f32[:]
-                )
+                for j in range(4):
+                    nc.tensor.matmul(
+                        out=pooled_half[:, fh, :],
+                        lhsT=sum4[:, j, P * fh : P * (fh + 1)],
+                        rhs=ident_f32[:],
+                        start=(j == 0),
+                        stop=(j == 3),
+                        is_transpose=True,
+                    )
 
         for te in range(TILES):
             n = te % CHUNK_TILES
@@ -199,10 +197,7 @@ def tile_fermilayer_pa_kernel(tc, h_one, h_two_same, h_two_diff, W1, b1, Wg, out
             cols = slice(P * n, P * (n + 1))
 
             pooled = psum_pair.tile([P, PACK, P], F32, name="pooled")
-            if te % 2 == 0:
-                sum_rows_by_adds(h_two_diff, te, pooled[:, 2:4, :])
-            else:
-                sum_rows_on_tensor_engine(h_two_diff, te, pooled[:, 2:4, :])
+            sum_rows_by_adds(h_two_diff, te, pooled[:, 2:4, :])
             sum_rows_on_tensor_engine(h_two_same, te, pooled[:, 0:2, :])
 
             pair_grouped = tile_pool.tile([P, P, PACK], BF16, name="pair_grouped", align_bytes=64)

@@ -14,17 +14,18 @@ MULT = mybir.AluOpType.mult
 
 P = 128
 PACK = 4
+PASSES = 4
 NSPIN = 8
 D_ONE = 512
 D_TWO = 256
 ELECTRONS = 2048
 TILES = ELECTRONS // P
-CHUNK_TILES = 4
-CHUNK = CHUNK_TILES * P
 TILE_GROUPS = P // NSPIN
-CHUNK_GROUPS = CHUNK // NSPIN
 UNIT_ROWS = P * NSPIN
-UNIT_BUFS = 20
+
+LOAD_AHEAD = 6
+QUANT_LAG = 2
+FINISH_LAG = 4
 
 TANH_GAIN = 1.5927812698663606
 INV_SQRT2 = 1.0 / math.sqrt(2.0)
@@ -35,22 +36,60 @@ FLOPS = 2 * (ELECTRONS + ELECTRONS // NSPIN) * 1024 * D_ONE
 def tile_fermilayer_pa_kernel(tc, h_one, h_two_same, h_two_diff, W1, b1, Wg, out):
     nc = tc.nc
     with ExitStack() as ctx:
+        ctx.enter_context(tc.manual_schedule())
         const = ctx.enter_context(tc.tile_pool(name="const", bufs=1))
         w_stage = ctx.enter_context(tc.tile_pool(name="w_stage", bufs=2))
-        h_pool = ctx.enter_context(tc.tile_pool(name="h_pool", bufs=TILES // CHUNK_TILES))
-        chunk_pool = ctx.enter_context(tc.tile_pool(name="chunk_pool", bufs=2))
-        units = ctx.enter_context(tc.tile_pool(name="units", bufs=UNIT_BUFS))
+        h_pool = ctx.enter_context(tc.tile_pool(name="h_pool", bufs=TILES))
+        units = ctx.enter_context(tc.tile_pool(name="units", bufs=2 * (LOAD_AHEAD + 2)))
         sums = ctx.enter_context(tc.tile_pool(name="sums", bufs=2))
-        tile_pool = ctx.enter_context(tc.tile_pool(name="tile_pool", bufs=3))
-        out_pool = ctx.enter_context(tc.tile_pool(name="out_pool", bufs=8))
+        grouped_pool = ctx.enter_context(tc.tile_pool(name="grouped_pool", bufs=QUANT_LAG + 2))
+        codes_pool = ctx.enter_context(tc.tile_pool(name="codes_pool", bufs=2))
+        z_pool = ctx.enter_context(tc.tile_pool(name="z_pool", bufs=2))
+        out_pool = ctx.enter_context(tc.tile_pool(name="out_pool", bufs=6))
         psum_t = ctx.enter_context(tc.psum_pool(name="psum_t", bufs=2))
         psum_g = ctx.enter_context(tc.psum_pool(name="psum_g", bufs=1))
         psum_pair = ctx.enter_context(tc.psum_pool(name="psum_pair", bufs=2))
         psum_acc = ctx.enter_context(tc.psum_pool(name="psum_acc", bufs=3))
 
+        h_tiles = {}
+        same_rows = {}
+        diff_rows = {}
+        grouped_tiles = {}
+        acc_tiles = {}
+        z_tiles = {}
+        result_tiles = {}
+
+        def load_tile(t):
+            h_nat = h_pool.tile([P, D_ONE], BF16, name="h_nat")
+            nc.sync.dma_start(out=h_nat[:], in_=h_one[P * t : P * (t + 1), :])
+            diff = units.tile([P, NSPIN, D_TWO], BF16, name="diff", tag="unit")
+            nc.sync.dma_start(
+                out=diff[:],
+                in_=h_two_diff[UNIT_ROWS * t : UNIT_ROWS * (t + 1), :].rearrange(
+                    "(p j) f -> p j f", j=NSPIN
+                ),
+            )
+            same = units.tile([P, NSPIN, D_TWO], BF16, name="same", tag="unit")
+            nc.sync.dma_start(
+                out=same[:],
+                in_=h_two_same[UNIT_ROWS * t : UNIT_ROWS * (t + 1), :].rearrange(
+                    "(r p) f -> p r f", p=P
+                ),
+            )
+            h_tiles[t] = h_nat
+            diff_rows[t] = diff
+            same_rows[t] = same
+
         b_row = const.tile([P, D_ONE], BF16, name="b_row")
         nc.vector.memset(b_row[:], 0.0)
         nc.sync.dma_start(out=b_row[0:1, :], in_=b1.rearrange("(r c) -> r c", r=1))
+        w_raw = []
+        for w_dram in (W1, Wg):
+            raw = w_stage.tile([P, 2 * PACK, D_ONE], BF16, name="w_raw")
+            nc.sync.dma_start(out=raw[:], in_=w_dram.rearrange("(c p) f -> p c f", p=P))
+            w_raw.append(raw)
+        for t in range(LOAD_AHEAD):
+            load_tile(t)
 
         ident_bf = const.tile([P, P], BF16, name="ident_bf")
         make_identity(nc, ident_bf[:])
@@ -73,17 +112,17 @@ def tile_fermilayer_pa_kernel(tc, h_one, h_two_same, h_two_diff, W1, b1, Wg, out
         b1_rep = const.tile([P, D_ONE], F32, name="b1_rep")
         nc.vector.tensor_copy(out=b1_rep[:], in_=b_rep_ps[:])
 
-        w_codes = const.tile([P, 4, D_ONE], U32, name="w_codes", align_bytes=64)
-        w_scales = const.tile([P, 4, D_ONE], U8, name="w_scales", align_bytes=64)
-        for w_index, w_dram in enumerate((W1, Wg)):
-            w_raw = w_stage.tile([P, 2 * PACK, D_ONE], BF16, name="w_raw")
-            nc.sync.dma_start(out=w_raw[:], in_=w_dram.rearrange("(c p) f -> p c f", p=P))
+        w_codes = const.tile([P, PASSES, D_ONE], U32, name="w_codes", align_bytes=64)
+        w_scales = const.tile([P, PASSES, D_ONE], U8, name="w_scales", align_bytes=64)
+        for w_index in range(2):
             grouped = []
             for half in range(2):
                 w_grouped = w_stage.tile([P, D_ONE, PACK], BF16, name="w_grouped", align_bytes=64)
                 nc.vector.tensor_copy(
-                    out=w_grouped[:],
-                    in_=w_raw[:, PACK * half : PACK * (half + 1), :].rearrange("p t f -> p f t"),
+                    out=w_grouped[:].rearrange("p (c i) t -> p c t i", i=4),
+                    in_=w_raw[w_index][:, PACK * half : PACK * (half + 1), :].rearrange(
+                        "p t (c i) -> p c t i", i=4
+                    ),
                 )
                 grouped.append(w_grouped)
             for half in range(2):
@@ -93,156 +132,135 @@ def tile_fermilayer_pa_kernel(tc, h_one, h_two_same, h_two_diff, W1, b1, Wg, out
                     in_=grouped[half][:].rearrange("p f t -> p (f t)"),
                 )
 
-        def prepare_chunk(q):
-            h_nat = h_pool.tile([P, CHUNK_TILES, D_ONE], BF16, name="h_nat")
-            nc.sync.dma_start(
-                out=h_nat[:],
-                in_=h_one[CHUNK * q : CHUNK * (q + 1), :].rearrange("(n p) f -> p n f", p=P),
-            )
-            x_codes = chunk_pool.tile([P, 3, CHUNK], U32, name="x_codes", align_bytes=64)
-            x_scales = chunk_pool.tile([P, 3, CHUNK], U8, name="x_scales", align_bytes=64)
-            h_grouped = chunk_pool.tile([P, CHUNK, PACK], BF16, name="h_grouped", align_bytes=64)
-            g_sum = psum_g.tile([P, PACK, CHUNK_GROUPS], F32, name="g_sum")
-            for n in range(CHUNK_TILES):
-                hT = psum_t.tile([P, PACK, P], BF16, name="hT", tag="hT")
-                for t in range(PACK):
-                    nc.tensor.transpose(hT[:, t, :], h_nat[:, n, P * t : P * (t + 1)], ident_bf[:])
-                nc.scalar.copy(
-                    out=h_grouped[:, P * n : P * (n + 1), :], in_=hT[:].rearrange("p t e -> p e t")
-                )
-                for t in range(PACK):
-                    nc.tensor.matmul(
-                        out=g_sum[:, t, TILE_GROUPS * n : TILE_GROUPS * (n + 1)],
-                        lhsT=h_nat[:, n, P * t : P * (t + 1)],
-                        rhs=pool_rows[:],
-                        start=True,
-                        stop=True,
-                    )
-            g_means = chunk_pool.tile([P, 2, CHUNK_GROUPS, PACK], BF16, name="g_means")
-            nc.scalar.mul(
-                out=g_means[:, 0, :, :], in_=g_sum[:].rearrange("p t g -> p g t"), mul=1.0 / NSPIN
-            )
-            partner = g_means[:, 1, :, :].rearrange("p (m s) t -> p m s t", s=2)
-            by_spin = g_sum[:].rearrange("p t (m s) -> p m s t", s=2)
-            for s in range(2):
-                nc.scalar.mul(out=partner[:, :, 1 - s, :], in_=by_spin[:, :, s, :], mul=1.0 / NSPIN)
-            repeated = []
-            for c in range(2):
-                g_rep = chunk_pool.tile(
-                    [P, CHUNK_GROUPS, NSPIN, PACK], BF16, name="g_rep", align_bytes=64
-                )
-                nc.vector.tensor_copy(
-                    out=g_rep[:],
-                    in_=g_means[:, c, :, :]
-                    .unsqueeze(2)
-                    .to_broadcast([P, CHUNK_GROUPS, NSPIN, PACK]),
-                )
-                repeated.append(g_rep)
-            nc.vector.quantize_mx(
-                out=x_codes[:, 0, :].bitcast(FP8X4),
-                scales=x_scales[:, 0, :],
-                in_=h_grouped[:].rearrange("p e t -> p (e t)"),
-            )
-            for c in range(2):
-                nc.vector.quantize_mx(
-                    out=x_codes[:, 1 + c, :].bitcast(FP8X4),
-                    scales=x_scales[:, 1 + c, :],
-                    in_=repeated[c][:].rearrange("p g i t -> p (g i t)"),
-                )
-            return h_nat, x_codes, x_scales
+        def sum_and_transpose(t):
+            h_nat = h_tiles[t]
+            same = same_rows[t]
+            diff = diff_rows[t]
+            grouped = grouped_pool.tile([P, PASSES, P, PACK], BF16, name="grouped", align_bytes=64)
+            grouped_tiles[t] = grouped
 
-        def sum_rows_on_tensor_engine(stream, te, pooled_half):
-            rows = units.tile([P, NSPIN, D_TWO], BF16, name="rows", tag="unit")
-            nc.sync.dma_start(
-                out=rows[:],
-                in_=stream[UNIT_ROWS * te : UNIT_ROWS * (te + 1), :].rearrange(
-                    "(r p) f -> p r f", p=P
-                ),
-            )
+            hT = psum_t.tile([P, PACK, P], BF16, name="hT")
+            for k in range(PACK):
+                nc.tensor.transpose(hT[:, k, :], h_nat[:, P * k : P * (k + 1)], ident_bf[:])
+            g_sum = psum_g.tile([P, PACK, TILE_GROUPS], F32, name="g_sum")
+            for k in range(PACK):
+                nc.tensor.matmul(
+                    out=g_sum[:, k, :],
+                    lhsT=h_nat[:, P * k : P * (k + 1)],
+                    rhs=pool_rows[:],
+                    start=True,
+                    stop=True,
+                )
+            pooled = psum_pair.tile([P, PACK, P], F32, name="pooled")
             for r in range(NSPIN):
                 for fh in range(2):
                     nc.tensor.matmul(
-                        out=pooled_half[:, fh, TILE_GROUPS * r : TILE_GROUPS * (r + 1)],
-                        lhsT=rows[:, r, P * fh : P * (fh + 1)],
+                        out=pooled[:, fh, TILE_GROUPS * r : TILE_GROUPS * (r + 1)],
+                        lhsT=same[:, r, P * fh : P * (fh + 1)],
                         rhs=pool_rows[:],
                         start=True,
                         stop=True,
                     )
 
-        def sum_rows_by_adds(stream, te, pooled_half):
-            rows = units.tile([P, NSPIN, D_TWO], BF16, name="rows", tag="unit")
-            nc.sync.dma_start(
-                out=rows[:],
-                in_=stream[UNIT_ROWS * te : UNIT_ROWS * (te + 1), :].rearrange(
-                    "(p j) f -> p j f", j=NSPIN
-                ),
-            )
             sum4 = sums.tile([P, 4, D_TWO], F32, name="sum4")
-            nc.vector.tensor_tensor(out=sum4[:], in0=rows[:, 0:4, :], in1=rows[:, 4:8, :], op=ADD)
+            nc.vector.tensor_tensor(out=sum4[:], in0=diff[:, 0:4, :], in1=diff[:, 4:8, :], op=ADD)
+
+            nc.scalar.copy(out=grouped[:, 0, :, :], in_=hT[:].rearrange("p k e -> p e k"))
+            g_means = sums.tile([P, TILE_GROUPS, PACK], BF16, name="g_means")
+            nc.scalar.mul(out=g_means[:], in_=g_sum[:].rearrange("p k g -> p g k"), mul=1.0 / NSPIN)
+
+            nc.gpsimd.tensor_scalar(
+                out=grouped[:, 2, :, :].rearrange("p (g i) k -> p g i k", i=NSPIN),
+                in0=g_means[:].unsqueeze(2).to_broadcast([P, TILE_GROUPS, NSPIN, PACK]),
+                scalar1=1.0,
+                scalar2=0.0,
+                op0=MULT,
+                op1=ADD,
+            )
+            partner_out = grouped[:, 3, :, :].rearrange("p (m s i) k -> p m s i k", s=2, i=NSPIN)
+            by_spin = g_means[:].rearrange("p (m s) k -> p m s k", s=2)
+            for s in range(2):
+                nc.gpsimd.tensor_scalar(
+                    out=partner_out[:, :, 1 - s, :, :],
+                    in0=by_spin[:, :, s, :]
+                    .unsqueeze(2)
+                    .to_broadcast([P, TILE_GROUPS // 2, NSPIN, PACK]),
+                    scalar1=1.0,
+                    scalar2=0.0,
+                    op0=MULT,
+                    op1=ADD,
+                )
+
             for fh in range(2):
                 for j in range(4):
                     nc.tensor.matmul(
-                        out=pooled_half[:, fh, :],
+                        out=pooled[:, 2 + fh, :],
                         lhsT=sum4[:, j, P * fh : P * (fh + 1)],
                         rhs=ident_f32[:],
                         start=(j == 0),
                         stop=(j == 3),
                         is_transpose=True,
                     )
-
-        for te in range(TILES):
-            n = te % CHUNK_TILES
-            if n == 0:
-                h_nat, x_codes, x_scales = prepare_chunk(te // CHUNK_TILES)
-            cols = slice(P * n, P * (n + 1))
-
-            pooled = psum_pair.tile([P, PACK, P], F32, name="pooled")
-            sum_rows_by_adds(h_two_diff, te, pooled[:, 2:4, :])
-            sum_rows_on_tensor_engine(h_two_same, te, pooled[:, 0:2, :])
-
-            pair_grouped = tile_pool.tile([P, P, PACK], BF16, name="pair_grouped", align_bytes=64)
             nc.scalar.mul(
-                out=pair_grouped[:], in_=pooled[:].rearrange("p t e -> p e t"), mul=1.0 / NSPIN
-            )
-            pair_codes = tile_pool.tile([P, P], U32, name="pair_codes", align_bytes=64)
-            pair_scales = tile_pool.tile([P, P], U8, name="pair_scales", align_bytes=64)
-            nc.vector.quantize_mx(
-                out=pair_codes[:].bitcast(FP8X4),
-                scales=pair_scales[:],
-                in_=pair_grouped[:].rearrange("p e t -> p (e t)"),
+                out=grouped[:, 1, :, :], in_=pooled[:].rearrange("p k e -> p e k"), mul=1.0 / NSPIN
             )
 
-            acc = psum_acc.tile([P, D_ONE], F32, name="acc", tag="acc")
-            passes = (
-                (x_codes[:, 0, cols], x_scales[:, 0, cols], 0),
-                (x_codes[:, 1, cols], x_scales[:, 1, cols], 2),
-                (x_codes[:, 2, cols], x_scales[:, 2, cols], 3),
-                (pair_codes[:], pair_scales[:], 1),
+        def quantise_and_multiply(t):
+            grouped = grouped_tiles[t]
+            codes = codes_pool.tile([P, PASSES, P], U32, name="codes", align_bytes=64)
+            scales = codes_pool.tile([P, PASSES, P], U8, name="scales", align_bytes=64)
+            nc.vector.quantize_mx(
+                out=codes[:].rearrange("p c e -> p (c e)").bitcast(FP8X4),
+                scales=scales[:].rearrange("p c e -> p (c e)"),
+                in_=grouped[:].rearrange("p c e k -> p (c e k)"),
             )
-            for i, (codes, scales, w) in enumerate(passes):
+            acc = psum_acc.tile([P, D_ONE], F32, name="acc", tag="acc")
+            acc_tiles[t] = acc
+            for c in range(PASSES):
                 nc.tensor.matmul_mx(
                     out=acc[:],
-                    lhsT=codes.bitcast(FP8X4),
-                    lhsT_scale=scales,
-                    rhs=w_codes[:, w, :].bitcast(FP8X4),
-                    rhs_scale=w_scales[:, w, :],
-                    start=(i == 0),
-                    stop=(i == len(passes) - 1),
+                    lhsT=codes[:, c, :].bitcast(FP8X4),
+                    lhsT_scale=scales[:, c, :],
+                    rhs=w_codes[:, c, :].bitcast(FP8X4),
+                    rhs_scale=w_scales[:, c, :],
+                    start=(c == 0),
+                    stop=(c == PASSES - 1),
                 )
 
-            z = tile_pool.tile([P, D_ONE], F32, name="z")
-            nc.vector.tensor_tensor(out=z[:], in0=acc[:], in1=b1_rep[:], op=ADD)
+        def bias_and_tanh(t):
+            z = z_pool.tile([P, D_ONE], F32, name="z")
+            z_tiles[t] = z
+            nc.vector.tensor_tensor(out=z[:], in0=acc_tiles[t][:], in1=b1_rep[:], op=ADD)
             nc.scalar.activation(
                 out=z[:], in_=z[:], func=mybir.ActivationFunctionType.Tanh, scale=INV_SQRT2
             )
             result = out_pool.tile([P, D_ONE], F32, name="result")
-            nc.scalar.mul(out=result[:], in_=h_nat[:, n, :], mul=INV_SQRT2)
+            result_tiles[t] = result
+            nc.scalar.mul(out=result[:], in_=h_tiles[t][:], mul=INV_SQRT2)
+
+        def residual_and_store(t):
+            result = result_tiles[t]
             nc.vector.scalar_tensor_tensor(
                 out=result[:],
-                in0=z[:],
+                in0=z_tiles[t][:],
                 scalar=TANH_GAIN * INV_SQRT2,
                 in1=result[:],
                 op0=MULT,
                 op1=ADD,
             )
-            nc.sync.dma_start(out=out[P * te : P * (te + 1), :], in_=result[:])
+            nc.sync.dma_start(out=out[P * t : P * (t + 1), :], in_=result[:])
+
+        def is_tile(t):
+            return 0 <= t < TILES
+
+        for i in range(TILES + FINISH_LAG):
+            if is_tile(i + LOAD_AHEAD):
+                load_tile(i + LOAD_AHEAD)
+            if is_tile(i - FINISH_LAG):
+                bias_and_tanh(i - FINISH_LAG)
+            if is_tile(i):
+                sum_and_transpose(i)
+            if is_tile(i - QUANT_LAG):
+                quantise_and_multiply(i - QUANT_LAG)
+            if is_tile(i - FINISH_LAG):
+                residual_and_store(i - FINISH_LAG)

@@ -14,18 +14,17 @@ MULT = mybir.AluOpType.mult
 
 P = 128
 PACK = 4
-PASSES = 4
 NSPIN = 8
 D_ONE = 512
 D_TWO = 256
 ELECTRONS = 2048
 TILES = ELECTRONS // P
+CHUNK_TILES = 4
+CHUNK = CHUNK_TILES * P
 TILE_GROUPS = P // NSPIN
+CHUNK_GROUPS = CHUNK // NSPIN
 UNIT_ROWS = P * NSPIN
-
-LOAD_AHEAD = 6
-QUANT_LAG = 2
-FINISH_LAG = 4
+UNIT_BUFS = 20
 
 TANH_GAIN = 1.5927812698663606
 INV_SQRT2 = 1.0 / math.sqrt(2.0)
@@ -36,60 +35,22 @@ FLOPS = 2 * (ELECTRONS + ELECTRONS // NSPIN) * 1024 * D_ONE
 def tile_fermilayer_pa_kernel(tc, h_one, h_two_same, h_two_diff, W1, b1, Wg, out):
     nc = tc.nc
     with ExitStack() as ctx:
-        ctx.enter_context(tc.manual_schedule())
         const = ctx.enter_context(tc.tile_pool(name="const", bufs=1))
         w_stage = ctx.enter_context(tc.tile_pool(name="w_stage", bufs=2))
-        h_pool = ctx.enter_context(tc.tile_pool(name="h_pool", bufs=TILES))
-        units = ctx.enter_context(tc.tile_pool(name="units", bufs=2 * (LOAD_AHEAD + 2)))
+        h_pool = ctx.enter_context(tc.tile_pool(name="h_pool", bufs=TILES // CHUNK_TILES))
+        chunk_pool = ctx.enter_context(tc.tile_pool(name="chunk_pool", bufs=2))
+        units = ctx.enter_context(tc.tile_pool(name="units", bufs=UNIT_BUFS))
         sums = ctx.enter_context(tc.tile_pool(name="sums", bufs=2))
-        grouped_pool = ctx.enter_context(tc.tile_pool(name="grouped_pool", bufs=QUANT_LAG + 2))
-        codes_pool = ctx.enter_context(tc.tile_pool(name="codes_pool", bufs=2))
-        z_pool = ctx.enter_context(tc.tile_pool(name="z_pool", bufs=2))
-        out_pool = ctx.enter_context(tc.tile_pool(name="out_pool", bufs=6))
+        tile_pool = ctx.enter_context(tc.tile_pool(name="tile_pool", bufs=3))
+        out_pool = ctx.enter_context(tc.tile_pool(name="out_pool", bufs=8))
         psum_t = ctx.enter_context(tc.psum_pool(name="psum_t", bufs=2))
         psum_g = ctx.enter_context(tc.psum_pool(name="psum_g", bufs=1))
         psum_pair = ctx.enter_context(tc.psum_pool(name="psum_pair", bufs=2))
         psum_acc = ctx.enter_context(tc.psum_pool(name="psum_acc", bufs=3))
 
-        h_tiles = {}
-        same_rows = {}
-        diff_rows = {}
-        grouped_tiles = {}
-        acc_tiles = {}
-        z_tiles = {}
-        result_tiles = {}
-
-        def load_tile(t):
-            h_nat = h_pool.tile([P, D_ONE], BF16, name="h_nat")
-            nc.sync.dma_start(out=h_nat[:], in_=h_one[P * t : P * (t + 1), :])
-            diff = units.tile([P, NSPIN, D_TWO], BF16, name="diff", tag="unit")
-            nc.sync.dma_start(
-                out=diff[:],
-                in_=h_two_diff[UNIT_ROWS * t : UNIT_ROWS * (t + 1), :].rearrange(
-                    "(p j) f -> p j f", j=NSPIN
-                ),
-            )
-            same = units.tile([P, NSPIN, D_TWO], BF16, name="same", tag="unit")
-            nc.sync.dma_start(
-                out=same[:],
-                in_=h_two_same[UNIT_ROWS * t : UNIT_ROWS * (t + 1), :].rearrange(
-                    "(r p) f -> p r f", p=P
-                ),
-            )
-            h_tiles[t] = h_nat
-            diff_rows[t] = diff
-            same_rows[t] = same
-
         b_row = const.tile([P, D_ONE], BF16, name="b_row")
         nc.vector.memset(b_row[:], 0.0)
         nc.sync.dma_start(out=b_row[0:1, :], in_=b1.rearrange("(r c) -> r c", r=1))
-        w_raw = []
-        for w_dram in (W1, Wg):
-            raw = w_stage.tile([P, 2 * PACK, D_ONE], BF16, name="w_raw")
-            nc.sync.dma_start(out=raw[:], in_=w_dram.rearrange("(c p) f -> p c f", p=P))
-            w_raw.append(raw)
-        for t in range(LOAD_AHEAD):
-            load_tile(t)
 
         ident_bf = const.tile([P, P], BF16, name="ident_bf")
         make_identity(nc, ident_bf[:])
@@ -112,17 +73,18 @@ def tile_fermilayer_pa_kernel(tc, h_one, h_two_same, h_two_diff, W1, b1, Wg, out
         b1_rep = const.tile([P, D_ONE], F32, name="b1_rep")
         nc.vector.tensor_copy(out=b1_rep[:], in_=b_rep_ps[:])
 
-        w_codes = const.tile([P, PASSES, D_ONE], U32, name="w_codes", align_bytes=64)
-        w_scales = const.tile([P, PASSES, D_ONE], U8, name="w_scales", align_bytes=64)
-        for w_index in range(2):
+        w_codes = const.tile([P, 4, D_ONE], U32, name="w_codes", align_bytes=64)
+        w_scales = const.tile([P, 4, D_ONE], U8, name="w_scales", align_bytes=64)
+        for w_index, w_dram in enumerate((W1, Wg)):
+            w_raw = w_stage.tile([P, 2 * PACK, D_ONE], BF16, name="w_raw")
+            nc.sync.dma_start(out=w_raw[:], in_=w_dram.rearrange("(c p) f -> p c f", p=P))
             grouped = []
             for half in range(2):
                 w_grouped = w_stage.tile([P, D_ONE, PACK], BF16, name="w_grouped", align_bytes=64)
-                nc.vector.tensor_copy(
-                    out=w_grouped[:].rearrange("p (c i) t -> p c t i", i=4),
-                    in_=w_raw[w_index][:, PACK * half : PACK * (half + 1), :].rearrange(
-                        "p t (c i) -> p c t i", i=4
-                    ),
+                regroup = (nc.vector.tensor_copy, nc.scalar.copy)[w_index]
+                regroup(
+                    out=w_grouped[:],
+                    in_=w_raw[:, PACK * half : PACK * (half + 1), :].rearrange("p t f -> p f t"),
                 )
                 grouped.append(w_grouped)
             for half in range(2):
@@ -132,135 +94,162 @@ def tile_fermilayer_pa_kernel(tc, h_one, h_two_same, h_two_diff, W1, b1, Wg, out
                     in_=grouped[half][:].rearrange("p f t -> p (f t)"),
                 )
 
-        def sum_and_transpose(t):
-            h_nat = h_tiles[t]
-            same = same_rows[t]
-            diff = diff_rows[t]
-            grouped = grouped_pool.tile([P, PASSES, P, PACK], BF16, name="grouped", align_bytes=64)
-            grouped_tiles[t] = grouped
-
-            hT = psum_t.tile([P, PACK, P], BF16, name="hT")
-            for k in range(PACK):
-                nc.tensor.transpose(hT[:, k, :], h_nat[:, P * k : P * (k + 1)], ident_bf[:])
-            g_sum = psum_g.tile([P, PACK, TILE_GROUPS], F32, name="g_sum")
-            for k in range(PACK):
-                nc.tensor.matmul(
-                    out=g_sum[:, k, :],
-                    lhsT=h_nat[:, P * k : P * (k + 1)],
-                    rhs=pool_rows[:],
-                    start=True,
-                    stop=True,
+        def prepare_chunk(q):
+            h_nat = h_pool.tile([P, CHUNK_TILES, D_ONE], BF16, name="h_nat")
+            nc.sync.dma_start(
+                out=h_nat[:],
+                in_=h_one[CHUNK * q : CHUNK * (q + 1), :].rearrange("(n p) f -> p n f", p=P),
+            )
+            x_codes = chunk_pool.tile([P, 3, CHUNK], U32, name="x_codes", align_bytes=64)
+            x_scales = chunk_pool.tile([P, 3, CHUNK], U8, name="x_scales", align_bytes=64)
+            h_grouped = chunk_pool.tile([P, CHUNK, PACK], BF16, name="h_grouped", align_bytes=64)
+            g_sum = psum_g.tile([P, PACK, CHUNK_GROUPS], F32, name="g_sum")
+            for n in range(CHUNK_TILES):
+                hT = psum_t.tile([P, PACK, P], BF16, name="hT", tag="hT")
+                for t in range(PACK):
+                    nc.tensor.transpose(hT[:, t, :], h_nat[:, n, P * t : P * (t + 1)], ident_bf[:])
+                nc.scalar.copy(
+                    out=h_grouped[:, P * n : P * (n + 1), :], in_=hT[:].rearrange("p t e -> p e t")
                 )
-            pooled = psum_pair.tile([P, PACK, P], F32, name="pooled")
-            for r in range(NSPIN):
-                for fh in range(2):
+                for t in range(PACK):
                     nc.tensor.matmul(
-                        out=pooled[:, fh, TILE_GROUPS * r : TILE_GROUPS * (r + 1)],
-                        lhsT=same[:, r, P * fh : P * (fh + 1)],
+                        out=g_sum[:, t, TILE_GROUPS * n : TILE_GROUPS * (n + 1)],
+                        lhsT=h_nat[:, n, P * t : P * (t + 1)],
                         rhs=pool_rows[:],
                         start=True,
                         stop=True,
                     )
-
-            sum4 = sums.tile([P, 4, D_TWO], F32, name="sum4")
-            nc.vector.tensor_tensor(out=sum4[:], in0=diff[:, 0:4, :], in1=diff[:, 4:8, :], op=ADD)
-
-            nc.scalar.copy(out=grouped[:, 0, :, :], in_=hT[:].rearrange("p k e -> p e k"))
-            g_means = sums.tile([P, TILE_GROUPS, PACK], BF16, name="g_means")
-            nc.scalar.mul(out=g_means[:], in_=g_sum[:].rearrange("p k g -> p g k"), mul=1.0 / NSPIN)
-
-            nc.gpsimd.tensor_scalar(
-                out=grouped[:, 2, :, :].rearrange("p (g i) k -> p g i k", i=NSPIN),
-                in0=g_means[:].unsqueeze(2).to_broadcast([P, TILE_GROUPS, NSPIN, PACK]),
-                scalar1=1.0,
-                scalar2=0.0,
-                op0=MULT,
-                op1=ADD,
+            g_means = chunk_pool.tile([P, 2, CHUNK_GROUPS, PACK], BF16, name="g_means")
+            nc.scalar.mul(
+                out=g_means[:, 0, :, :], in_=g_sum[:].rearrange("p t g -> p g t"), mul=1.0 / NSPIN
             )
-            partner_out = grouped[:, 3, :, :].rearrange("p (m s i) k -> p m s i k", s=2, i=NSPIN)
-            by_spin = g_means[:].rearrange("p (m s) k -> p m s k", s=2)
+            partner = g_means[:, 1, :, :].rearrange("p (m s) t -> p m s t", s=2)
+            by_spin = g_sum[:].rearrange("p t (m s) -> p m s t", s=2)
             for s in range(2):
+                nc.scalar.mul(out=partner[:, :, 1 - s, :], in_=by_spin[:, :, s, :], mul=1.0 / NSPIN)
+            repeated = []
+            for c in range(2):
+                g_rep = chunk_pool.tile(
+                    [P, CHUNK_GROUPS, NSPIN, PACK], BF16, name="g_rep", align_bytes=64
+                )
                 nc.gpsimd.tensor_scalar(
-                    out=partner_out[:, :, 1 - s, :, :],
-                    in0=by_spin[:, :, s, :]
+                    out=g_rep[:],
+                    in0=g_means[:, c, :, :]
                     .unsqueeze(2)
-                    .to_broadcast([P, TILE_GROUPS // 2, NSPIN, PACK]),
+                    .to_broadcast([P, CHUNK_GROUPS, NSPIN, PACK]),
                     scalar1=1.0,
                     scalar2=0.0,
                     op0=MULT,
                     op1=ADD,
                 )
+                repeated.append(g_rep)
+            nc.vector.quantize_mx(
+                out=x_codes[:, 0, :].bitcast(FP8X4),
+                scales=x_scales[:, 0, :],
+                in_=h_grouped[:].rearrange("p e t -> p (e t)"),
+            )
+            for c in range(2):
+                nc.vector.quantize_mx(
+                    out=x_codes[:, 1 + c, :].bitcast(FP8X4),
+                    scales=x_scales[:, 1 + c, :],
+                    in_=repeated[c][:].rearrange("p g i t -> p (g i t)"),
+                )
+            return h_nat, x_codes, x_scales
 
-            for fh in range(2):
-                for j in range(4):
+        def sum_rows_on_tensor_engine(stream, te, pooled_half):
+            rows = units.tile([P, NSPIN, D_TWO], BF16, name="rows", tag="unit")
+            nc.sync.dma_start(
+                out=rows[:],
+                in_=stream[UNIT_ROWS * te : UNIT_ROWS * (te + 1), :].rearrange(
+                    "(r p) f -> p r f", p=P
+                ),
+            )
+            for r in range(NSPIN):
+                for fh in range(2):
                     nc.tensor.matmul(
-                        out=pooled[:, 2 + fh, :],
-                        lhsT=sum4[:, j, P * fh : P * (fh + 1)],
+                        out=pooled_half[:, fh, TILE_GROUPS * r : TILE_GROUPS * (r + 1)],
+                        lhsT=rows[:, r, P * fh : P * (fh + 1)],
+                        rhs=pool_rows[:],
+                        start=True,
+                        stop=True,
+                    )
+
+        def sum_rows_by_adds(stream, te, pooled_half):
+            rows = units.tile([P, NSPIN, D_TWO], BF16, name="rows", tag="unit")
+            nc.sync.dma_start(
+                out=rows[:],
+                in_=stream[UNIT_ROWS * te : UNIT_ROWS * (te + 1), :].rearrange(
+                    "(p j) f -> p j f", j=NSPIN
+                ),
+            )
+            sum4 = sums.tile([P, 4, D_TWO], F32, name="sum4")
+            nc.vector.tensor_tensor(out=sum4[:], in0=rows[:, 0:4, :], in1=rows[:, 4:8, :], op=ADD)
+            sum2 = sums.tile([P, 2, D_TWO], F32, name="sum2")
+            nc.vector.tensor_tensor(out=sum2[:], in0=sum4[:, 0:2, :], in1=sum4[:, 2:4, :], op=ADD)
+            for fh in range(2):
+                for j in range(2):
+                    nc.tensor.matmul(
+                        out=pooled_half[:, fh, :],
+                        lhsT=sum2[:, j, P * fh : P * (fh + 1)],
                         rhs=ident_f32[:],
                         start=(j == 0),
-                        stop=(j == 3),
+                        stop=(j == 1),
                         is_transpose=True,
                     )
+
+        for te in range(TILES):
+            n = te % CHUNK_TILES
+            if n == 0:
+                h_nat, x_codes, x_scales = prepare_chunk(te // CHUNK_TILES)
+            cols = slice(P * n, P * (n + 1))
+
+            pooled = psum_pair.tile([P, PACK, P], F32, name="pooled")
+            sum_rows_by_adds(h_two_diff, te, pooled[:, 2:4, :])
+            sum_rows_on_tensor_engine(h_two_same, te, pooled[:, 0:2, :])
+
+            pair_grouped = tile_pool.tile([P, P, PACK], BF16, name="pair_grouped", align_bytes=64)
             nc.scalar.mul(
-                out=grouped[:, 1, :, :], in_=pooled[:].rearrange("p k e -> p e k"), mul=1.0 / NSPIN
+                out=pair_grouped[:], in_=pooled[:].rearrange("p t e -> p e t"), mul=1.0 / NSPIN
+            )
+            pair_codes = tile_pool.tile([P, P], U32, name="pair_codes", align_bytes=64)
+            pair_scales = tile_pool.tile([P, P], U8, name="pair_scales", align_bytes=64)
+            nc.vector.quantize_mx(
+                out=pair_codes[:].bitcast(FP8X4),
+                scales=pair_scales[:],
+                in_=pair_grouped[:].rearrange("p e t -> p (e t)"),
             )
 
-        def quantise_and_multiply(t):
-            grouped = grouped_tiles[t]
-            codes = codes_pool.tile([P, PASSES, P], U32, name="codes", align_bytes=64)
-            scales = codes_pool.tile([P, PASSES, P], U8, name="scales", align_bytes=64)
-            nc.vector.quantize_mx(
-                out=codes[:].rearrange("p c e -> p (c e)").bitcast(FP8X4),
-                scales=scales[:].rearrange("p c e -> p (c e)"),
-                in_=grouped[:].rearrange("p c e k -> p (c e k)"),
-            )
             acc = psum_acc.tile([P, D_ONE], F32, name="acc", tag="acc")
-            acc_tiles[t] = acc
-            for c in range(PASSES):
+            passes = (
+                (x_codes[:, 0, cols], x_scales[:, 0, cols], 0),
+                (x_codes[:, 1, cols], x_scales[:, 1, cols], 2),
+                (x_codes[:, 2, cols], x_scales[:, 2, cols], 3),
+                (pair_codes[:], pair_scales[:], 1),
+            )
+            for i, (codes, scales, w) in enumerate(passes):
                 nc.tensor.matmul_mx(
                     out=acc[:],
-                    lhsT=codes[:, c, :].bitcast(FP8X4),
-                    lhsT_scale=scales[:, c, :],
-                    rhs=w_codes[:, c, :].bitcast(FP8X4),
-                    rhs_scale=w_scales[:, c, :],
-                    start=(c == 0),
-                    stop=(c == PASSES - 1),
+                    lhsT=codes.bitcast(FP8X4),
+                    lhsT_scale=scales,
+                    rhs=w_codes[:, w, :].bitcast(FP8X4),
+                    rhs_scale=w_scales[:, w, :],
+                    start=(i == 0),
+                    stop=(i == len(passes) - 1),
                 )
 
-        def bias_and_tanh(t):
-            z = z_pool.tile([P, D_ONE], F32, name="z")
-            z_tiles[t] = z
-            nc.vector.tensor_tensor(out=z[:], in0=acc_tiles[t][:], in1=b1_rep[:], op=ADD)
+            z = tile_pool.tile([P, D_ONE], F32, name="z")
+            nc.vector.tensor_tensor(out=z[:], in0=acc[:], in1=b1_rep[:], op=ADD)
             nc.scalar.activation(
                 out=z[:], in_=z[:], func=mybir.ActivationFunctionType.Tanh, scale=INV_SQRT2
             )
             result = out_pool.tile([P, D_ONE], F32, name="result")
-            result_tiles[t] = result
-            nc.scalar.mul(out=result[:], in_=h_tiles[t][:], mul=INV_SQRT2)
-
-        def residual_and_store(t):
-            result = result_tiles[t]
+            nc.scalar.mul(out=result[:], in_=h_nat[:, n, :], mul=INV_SQRT2)
             nc.vector.scalar_tensor_tensor(
                 out=result[:],
-                in0=z_tiles[t][:],
+                in0=z[:],
                 scalar=TANH_GAIN * INV_SQRT2,
                 in1=result[:],
                 op0=MULT,
                 op1=ADD,
             )
-            nc.sync.dma_start(out=out[P * t : P * (t + 1), :], in_=result[:])
-
-        def is_tile(t):
-            return 0 <= t < TILES
-
-        for i in range(TILES + FINISH_LAG):
-            if is_tile(i + LOAD_AHEAD):
-                load_tile(i + LOAD_AHEAD)
-            if is_tile(i - FINISH_LAG):
-                bias_and_tanh(i - FINISH_LAG)
-            if is_tile(i):
-                sum_and_transpose(i)
-            if is_tile(i - QUANT_LAG):
-                quantise_and_multiply(i - QUANT_LAG)
-            if is_tile(i - FINISH_LAG):
-                residual_and_store(i - FINISH_LAG)
+            nc.sync.dma_start(out=out[P * te : P * (te + 1), :], in_=result[:])

@@ -132,15 +132,11 @@ def tile_fermilayer_pa_kernel(tc, h_one, h_two_same, h_two_diff, W1, b1, Wg, out
                 g_rep = chunk_pool.tile(
                     [P, CHUNK_GROUPS, NSPIN, PACK], BF16, name="g_rep", align_bytes=64
                 )
-                nc.gpsimd.tensor_scalar(
+                nc.scalar.copy(
                     out=g_rep[:],
-                    in0=g_means[:, c, :, :]
+                    in_=g_means[:, c, :, :]
                     .unsqueeze(2)
                     .to_broadcast([P, CHUNK_GROUPS, NSPIN, PACK]),
-                    scalar1=1.0,
-                    scalar2=0.0,
-                    op0=MULT,
-                    op1=ADD,
                 )
                 repeated.append(g_rep)
             nc.vector.quantize_mx(

@@ -14,17 +14,18 @@ MULT = mybir.AluOpType.mult
 
 P = 128
 PACK = 4
+PASSES = 4
 NSPIN = 8
 D_ONE = 512
 D_TWO = 256
 ELECTRONS = 2048
 TILES = ELECTRONS // P
-CHUNK_TILES = 4
-CHUNK = CHUNK_TILES * P
 TILE_GROUPS = P // NSPIN
-CHUNK_GROUPS = CHUNK // NSPIN
 UNIT_ROWS = P * NSPIN
-UNIT_BUFS = 20
+
+LOAD_AHEAD = 6
+QUANT_LAG = 2
+FINISH_LAG = 4
 
 TANH_GAIN = 1.5927812698663606
 INV_SQRT2 = 1.0 / math.sqrt(2.0)
@@ -35,22 +36,60 @@ FLOPS = 2 * (ELECTRONS + ELECTRONS // NSPIN) * 1024 * D_ONE
 def tile_fermilayer_pa_kernel(tc, h_one, h_two_same, h_two_diff, W1, b1, Wg, out):
     nc = tc.nc
     with ExitStack() as ctx:
+        ctx.enter_context(tc.manual_schedule())
         const = ctx.enter_context(tc.tile_pool(name="const", bufs=1))
         w_stage = ctx.enter_context(tc.tile_pool(name="w_stage", bufs=2))
-        h_pool = ctx.enter_context(tc.tile_pool(name="h_pool", bufs=TILES // CHUNK_TILES))
-        chunk_pool = ctx.enter_context(tc.tile_pool(name="chunk_pool", bufs=2))
-        units = ctx.enter_context(tc.tile_pool(name="units", bufs=UNIT_BUFS))
+        h_pool = ctx.enter_context(tc.tile_pool(name="h_pool", bufs=TILES))
+        units = ctx.enter_context(tc.tile_pool(name="units", bufs=2 * (LOAD_AHEAD + 2)))
         sums = ctx.enter_context(tc.tile_pool(name="sums", bufs=2))
-        tile_pool = ctx.enter_context(tc.tile_pool(name="tile_pool", bufs=3))
-        out_pool = ctx.enter_context(tc.tile_pool(name="out_pool", bufs=8))
+        grouped_pool = ctx.enter_context(tc.tile_pool(name="grouped_pool", bufs=QUANT_LAG + 2))
+        codes_pool = ctx.enter_context(tc.tile_pool(name="codes_pool", bufs=2))
+        z_pool = ctx.enter_context(tc.tile_pool(name="z_pool", bufs=2))
+        out_pool = ctx.enter_context(tc.tile_pool(name="out_pool", bufs=6))
         psum_t = ctx.enter_context(tc.psum_pool(name="psum_t", bufs=2))
         psum_g = ctx.enter_context(tc.psum_pool(name="psum_g", bufs=1))
         psum_pair = ctx.enter_context(tc.psum_pool(name="psum_pair", bufs=2))
         psum_acc = ctx.enter_context(tc.psum_pool(name="psum_acc", bufs=3))
 
+        h_tiles = {}
+        same_rows = {}
+        diff_rows = {}
+        grouped_tiles = {}
+        acc_tiles = {}
+        z_tiles = {}
+        result_tiles = {}
+
+        def load_tile(t):
+            h_nat = h_pool.tile([P, D_ONE], BF16, name="h_nat")
+            nc.sync.dma_start(out=h_nat[:], in_=h_one[P * t : P * (t + 1), :])
+            diff = units.tile([P, NSPIN, D_TWO], BF16, name="diff", tag="unit")
+            nc.sync.dma_start(
+                out=diff[:],
+                in_=h_two_diff[UNIT_ROWS * t : UNIT_ROWS * (t + 1), :].rearrange(
+                    "(p j) f -> p j f", j=NSPIN
+                ),
+            )
+            same = units.tile([P, NSPIN, D_TWO], BF16, name="same", tag="unit")
+            nc.sync.dma_start(
+                out=same[:],
+                in_=h_two_same[UNIT_ROWS * t : UNIT_ROWS * (t + 1), :].rearrange(
+                    "(r p) f -> p r f", p=P
+                ),
+            )
+            h_tiles[t] = h_nat
+            diff_rows[t] = diff
+            same_rows[t] = same
+
         b_row = const.tile([P, D_ONE], BF16, name="b_row")
         nc.vector.memset(b_row[:], 0.0)
         nc.sync.dma_start(out=b_row[0:1, :], in_=b1.rearrange("(r c) -> r c", r=1))
+        w_raw = []
+        for w_dram in (W1, Wg):
+            raw = w_stage.tile([P, 2 * PACK, D_ONE], BF16, name="w_raw")
+            nc.sync.dma_start(out=raw[:], in_=w_dram.rearrange("(c p) f -> p c f", p=P))
+            w_raw.append(raw)
+        for t in range(LOAD_AHEAD):
+            load_tile(t)
 
         ident_bf = const.tile([P, P], BF16, name="ident_bf")
         make_identity(nc, ident_bf[:])
@@ -73,18 +112,17 @@ def tile_fermilayer_pa_kernel(tc, h_one, h_two_same, h_two_diff, W1, b1, Wg, out
         b1_rep = const.tile([P, D_ONE], F32, name="b1_rep")
         nc.vector.tensor_copy(out=b1_rep[:], in_=b_rep_ps[:])
 
-        w_codes = const.tile([P, 4, D_ONE], U32, name="w_codes", align_bytes=64)
-        w_scales = const.tile([P, 4, D_ONE], U8, name="w_scales", align_bytes=64)
-        for w_index, w_dram in enumerate((W1, Wg)):
-            w_raw = w_stage.tile([P, 2 * PACK, D_ONE], BF16, name="w_raw")
-            nc.sync.dma_start(out=w_raw[:], in_=w_dram.rearrange("(c p) f -> p c f", p=P))
+        w_codes = const.tile([P, PASSES, D_ONE], U32, name="w_codes", align_bytes=64)
+        w_scales = const.tile([P, PASSES, D_ONE], U8, name="w_scales", align_bytes=64)
+        for w_index in range(2):
             grouped = []
             for half in range(2):
                 w_grouped = w_stage.tile([P, D_ONE, PACK], BF16, name="w_grouped", align_bytes=64)
-                regroup = (nc.vector.tensor_copy, nc.scalar.copy)[w_index]
-                regroup(
-                    out=w_grouped[:],
-                    in_=w_raw[:, PACK * half : PACK * (half + 1), :].rearrange("p t f -> p f t"),
+                nc.vector.tensor_copy(
+                    out=w_grouped[:].rearrange("p (c i) t -> p c t i", i=4),
+                    in_=w_raw[w_index][:, PACK * half : PACK * (half + 1), :].rearrange(
+                        "p t (c i) -> p c t i", i=4
+                    ),
                 )
                 grouped.append(w_grouped)
             for half in range(2):
@@ -94,158 +132,127 @@ def tile_fermilayer_pa_kernel(tc, h_one, h_two_same, h_two_diff, W1, b1, Wg, out
                     in_=grouped[half][:].rearrange("p f t -> p (f t)"),
                 )
 
-        def prepare_chunk(q):
-            h_nat = h_pool.tile([P, CHUNK_TILES, D_ONE], BF16, name="h_nat")
-            nc.sync.dma_start(
-                out=h_nat[:],
-                in_=h_one[CHUNK * q : CHUNK * (q + 1), :].rearrange("(n p) f -> p n f", p=P),
-            )
-            x_codes = chunk_pool.tile([P, 3, CHUNK], U32, name="x_codes", align_bytes=64)
-            x_scales = chunk_pool.tile([P, 3, CHUNK], U8, name="x_scales", align_bytes=64)
-            h_grouped = chunk_pool.tile([P, CHUNK, PACK], BF16, name="h_grouped", align_bytes=64)
-            g_sum = psum_g.tile([P, PACK, CHUNK_GROUPS], F32, name="g_sum")
-            for n in range(CHUNK_TILES):
-                hT = psum_t.tile([P, PACK, P], BF16, name="hT", tag="hT")
-                for t in range(PACK):
-                    nc.tensor.transpose(hT[:, t, :], h_nat[:, n, P * t : P * (t + 1)], ident_bf[:])
-                nc.scalar.copy(
-                    out=h_grouped[:, P * n : P * (n + 1), :], in_=hT[:].rearrange("p t e -> p e t")
-                )
-                for t in range(PACK):
-                    nc.tensor.matmul(
-                        out=g_sum[:, t, TILE_GROUPS * n : TILE_GROUPS * (n + 1)],
-                        lhsT=h_nat[:, n, P * t : P * (t + 1)],
-                        rhs=pool_rows[:],
-                        start=True,
-                        stop=True,
-                    )
-            g_means = chunk_pool.tile([P, 2, CHUNK_GROUPS, PACK], BF16, name="g_means")
-            nc.scalar.mul(
-                out=g_means[:, 0, :, :], in_=g_sum[:].rearrange("p t g -> p g t"), mul=1.0 / NSPIN
-            )
-            partner = g_means[:, 1, :, :].rearrange("p (m s) t -> p m s t", s=2)
-            by_spin = g_sum[:].rearrange("p t (m s) -> p m s t", s=2)
-            for s in range(2):
-                nc.scalar.mul(out=partner[:, :, 1 - s, :], in_=by_spin[:, :, s, :], mul=1.0 / NSPIN)
-            repeated = []
-            for c in range(2):
-                g_rep = chunk_pool.tile(
-                    [P, CHUNK_GROUPS, NSPIN, PACK], BF16, name="g_rep", align_bytes=64
-                )
-                nc.scalar.copy(
-                    out=g_rep[:],
-                    in_=g_means[:, c, :, :]
-                    .unsqueeze(2)
-                    .to_broadcast([P, CHUNK_GROUPS, NSPIN, PACK]),
-                )
-                repeated.append(g_rep)
-            nc.vector.quantize_mx(
-                out=x_codes[:, 0, :].bitcast(FP8X4),
-                scales=x_scales[:, 0, :],
-                in_=h_grouped[:].rearrange("p e t -> p (e t)"),
-            )
-            for c in range(2):
-                nc.vector.quantize_mx(
-                    out=x_codes[:, 1 + c, :].bitcast(FP8X4),
-                    scales=x_scales[:, 1 + c, :],
-                    in_=repeated[c][:].rearrange("p g i t -> p (g i t)"),
-                )
-            return h_nat, x_codes, x_scales
+        def sum_and_transpose(t):
+            h_nat = h_tiles[t]
+            same = same_rows[t]
+            diff = diff_rows[t]
+            grouped = grouped_pool.tile([P, PASSES, P, PACK], BF16, name="grouped", align_bytes=64)
+            grouped_tiles[t] = grouped
 
-        def sum_rows_on_tensor_engine(stream, te, pooled_half):
-            rows = units.tile([P, NSPIN, D_TWO], BF16, name="rows", tag="unit")
-            nc.sync.dma_start(
-                out=rows[:],
-                in_=stream[UNIT_ROWS * te : UNIT_ROWS * (te + 1), :].rearrange(
-                    "(r p) f -> p r f", p=P
-                ),
-            )
+            hT = psum_t.tile([P, PACK, P], BF16, name="hT")
+            for k in range(PACK):
+                nc.tensor.transpose(hT[:, k, :], h_nat[:, P * k : P * (k + 1)], ident_bf[:])
+            g_sum = psum_g.tile([P, PACK, TILE_GROUPS], F32, name="g_sum")
+            for k in range(PACK):
+                nc.tensor.matmul(
+                    out=g_sum[:, k, :],
+                    lhsT=h_nat[:, P * k : P * (k + 1)],
+                    rhs=pool_rows[:],
+                    start=True,
+                    stop=True,
+                )
+            pooled = psum_pair.tile([P, PACK, P], F32, name="pooled")
             for r in range(NSPIN):
                 for fh in range(2):
                     nc.tensor.matmul(
-                        out=pooled_half[:, fh, TILE_GROUPS * r : TILE_GROUPS * (r + 1)],
-                        lhsT=rows[:, r, P * fh : P * (fh + 1)],
+                        out=pooled[:, fh, TILE_GROUPS * r : TILE_GROUPS * (r + 1)],
+                        lhsT=same[:, r, P * fh : P * (fh + 1)],
                         rhs=pool_rows[:],
                         start=True,
                         stop=True,
                     )
 
-        def sum_rows_by_adds(stream, te, pooled_half):
-            rows = units.tile([P, NSPIN, D_TWO], BF16, name="rows", tag="unit")
-            nc.sync.dma_start(
-                out=rows[:],
-                in_=stream[UNIT_ROWS * te : UNIT_ROWS * (te + 1), :].rearrange(
-                    "(p j) f -> p j f", j=NSPIN
-                ),
-            )
             sum4 = sums.tile([P, 4, D_TWO], F32, name="sum4")
-            nc.vector.tensor_tensor(out=sum4[:], in0=rows[:, 0:4, :], in1=rows[:, 4:8, :], op=ADD)
-            sum2 = sums.tile([P, 2, D_TWO], F32, name="sum2")
-            nc.vector.tensor_tensor(out=sum2[:], in0=sum4[:, 0:2, :], in1=sum4[:, 2:4, :], op=ADD)
-            for fh in range(2):
-                for j in range(2):
-                    nc.tensor.matmul(
-                        out=pooled_half[:, fh, :],
-                        lhsT=sum2[:, j, P * fh : P * (fh + 1)],
-                        rhs=ident_f32[:],
-                        start=(j == 0),
-                        stop=(j == 1),
-                        is_transpose=True,
-                    )
+            nc.vector.tensor_tensor(out=sum4[:], in0=diff[:, 0:4, :], in1=diff[:, 4:8, :], op=ADD)
 
-        for te in range(TILES):
-            n = te % CHUNK_TILES
-            if n == 0:
-                h_nat, x_codes, x_scales = prepare_chunk(te // CHUNK_TILES)
-            cols = slice(P * n, P * (n + 1))
-
-            pooled = psum_pair.tile([P, PACK, P], F32, name="pooled")
-            sum_rows_by_adds(h_two_diff, te, pooled[:, 2:4, :])
-            sum_rows_on_tensor_engine(h_two_same, te, pooled[:, 0:2, :])
-
-            pair_grouped = tile_pool.tile([P, P, PACK], BF16, name="pair_grouped", align_bytes=64)
+            nc.scalar.copy(out=grouped[:, 0, :, :], in_=hT[:].rearrange("p k e -> p e k"))
+            by_group = g_sum[:].rearrange("p k g -> p g k")
             nc.scalar.mul(
-                out=pair_grouped[:], in_=pooled[:].rearrange("p t e -> p e t"), mul=1.0 / NSPIN
+                out=grouped[:, 2, :, :].rearrange("p (g i) k -> p g i k", i=NSPIN),
+                in_=by_group.unsqueeze(2).to_broadcast([P, TILE_GROUPS, NSPIN, PACK]),
+                mul=1.0 / NSPIN,
             )
-            pair_codes = tile_pool.tile([P, P], U32, name="pair_codes", align_bytes=64)
-            pair_scales = tile_pool.tile([P, P], U8, name="pair_scales", align_bytes=64)
-            nc.vector.quantize_mx(
-                out=pair_codes[:].bitcast(FP8X4),
-                scales=pair_scales[:],
-                in_=pair_grouped[:].rearrange("p e t -> p (e t)"),
-            )
-
-            acc = psum_acc.tile([P, D_ONE], F32, name="acc", tag="acc")
-            passes = (
-                (x_codes[:, 0, cols], x_scales[:, 0, cols], 0),
-                (x_codes[:, 1, cols], x_scales[:, 1, cols], 2),
-                (x_codes[:, 2, cols], x_scales[:, 2, cols], 3),
-                (pair_codes[:], pair_scales[:], 1),
-            )
-            for i, (codes, scales, w) in enumerate(passes):
-                nc.tensor.matmul_mx(
-                    out=acc[:],
-                    lhsT=codes.bitcast(FP8X4),
-                    lhsT_scale=scales,
-                    rhs=w_codes[:, w, :].bitcast(FP8X4),
-                    rhs_scale=w_scales[:, w, :],
-                    start=(i == 0),
-                    stop=(i == len(passes) - 1),
+            partner_out = grouped[:, 3, :, :].rearrange("p (m s i) k -> p m s i k", s=2, i=NSPIN)
+            by_spin = g_sum[:].rearrange("p k (m s) -> p m s k", s=2)
+            for s in range(2):
+                nc.scalar.mul(
+                    out=partner_out[:, :, 1 - s, :, :],
+                    in_=by_spin[:, :, s, :]
+                    .unsqueeze(2)
+                    .to_broadcast([P, TILE_GROUPS // 2, NSPIN, PACK]),
+                    mul=1.0 / NSPIN,
                 )
 
-            z = tile_pool.tile([P, D_ONE], F32, name="z")
-            nc.vector.tensor_tensor(out=z[:], in0=acc[:], in1=b1_rep[:], op=ADD)
+            for fh in range(2):
+                for j in range(4):
+                    nc.tensor.matmul(
+                        out=pooled[:, 2 + fh, :],
+                        lhsT=sum4[:, j, P * fh : P * (fh + 1)],
+                        rhs=ident_f32[:],
+                        start=(j == 0),
+                        stop=(j == 3),
+                        is_transpose=True,
+                    )
+            nc.scalar.mul(
+                out=grouped[:, 1, :, :], in_=pooled[:].rearrange("p k e -> p e k"), mul=1.0 / NSPIN
+            )
+
+        def quantise_and_multiply(t):
+            grouped = grouped_tiles[t]
+            codes = codes_pool.tile([P, PASSES, P], U32, name="codes", align_bytes=64)
+            scales = codes_pool.tile([P, PASSES, P], U8, name="scales", align_bytes=64)
+            nc.vector.quantize_mx(
+                out=codes[:].rearrange("p c e -> p (c e)").bitcast(FP8X4),
+                scales=scales[:].rearrange("p c e -> p (c e)"),
+                in_=grouped[:].rearrange("p c e k -> p (c e k)"),
+            )
+            acc = psum_acc.tile([P, D_ONE], F32, name="acc", tag="acc")
+            acc_tiles[t] = acc
+            for c in range(PASSES):
+                nc.tensor.matmul_mx(
+                    out=acc[:],
+                    lhsT=codes[:, c, :].bitcast(FP8X4),
+                    lhsT_scale=scales[:, c, :],
+                    rhs=w_codes[:, c, :].bitcast(FP8X4),
+                    rhs_scale=w_scales[:, c, :],
+                    start=(c == 0),
+                    stop=(c == PASSES - 1),
+                )
+
+        def bias_and_tanh(t):
+            z = z_pool.tile([P, D_ONE], F32, name="z")
+            z_tiles[t] = z
+            nc.vector.tensor_tensor(out=z[:], in0=acc_tiles[t][:], in1=b1_rep[:], op=ADD)
             nc.scalar.activation(
                 out=z[:], in_=z[:], func=mybir.ActivationFunctionType.Tanh, scale=INV_SQRT2
             )
             result = out_pool.tile([P, D_ONE], F32, name="result")
-            nc.scalar.mul(out=result[:], in_=h_nat[:, n, :], mul=INV_SQRT2)
+            result_tiles[t] = result
+            nc.scalar.mul(out=result[:], in_=h_tiles[t][:], mul=INV_SQRT2)
+
+        def residual_and_store(t):
+            result = result_tiles[t]
             nc.vector.scalar_tensor_tensor(
                 out=result[:],
-                in0=z[:],
+                in0=z_tiles[t][:],
                 scalar=TANH_GAIN * INV_SQRT2,
                 in1=result[:],
                 op0=MULT,
                 op1=ADD,
             )
-            nc.sync.dma_start(out=out[P * te : P * (te + 1), :], in_=result[:])
+            nc.sync.dma_start(out=out[P * t : P * (t + 1), :], in_=result[:])
+
+        def is_tile(t):
+            return 0 <= t < TILES
+
+        for i in range(TILES + FINISH_LAG):
+            if is_tile(i + LOAD_AHEAD):
+                load_tile(i + LOAD_AHEAD)
+            if is_tile(i - FINISH_LAG):
+                bias_and_tanh(i - FINISH_LAG)
+            if is_tile(i):
+                sum_and_transpose(i)
+            if is_tile(i - QUANT_LAG):
+                quantise_and_multiply(i - QUANT_LAG)
+            if is_tile(i - FINISH_LAG):
+                residual_and_store(i - FINISH_LAG)

@@ -11,21 +11,28 @@ U8 = mybir.dt.uint8
 FP8X4 = mybir.dt.float8_e4m3fn_x4
 ADD = mybir.AluOpType.add
 MULT = mybir.AluOpType.mult
+ACT = mybir.ActivationFunctionType
 
 P = 128
 PACK = 4
-PASSES = 4
 NSPIN = 8
 D_ONE = 512
 D_TWO = 256
 ELECTRONS = 2048
 TILES = ELECTRONS // P
+GROUPS = ELECTRONS // NSPIN
 TILE_GROUPS = P // NSPIN
-UNIT_ROWS = P * NSPIN
+TILE_ROWS = P * NSPIN
+CHUNK_ROWS = 2
+CHUNKS = TILE_ROWS // (P * CHUNK_ROWS)
+CHUNK_COLS = P // CHUNKS
+H_SET = 4
+PAIR_SETS = 2
 
-LOAD_AHEAD = 6
-QUANT_LAG = 2
-FINISH_LAG = 4
+MATMUL_UNITS = {(t, 0) for t in range(TILES) if t % 3 != 1} | {(TILES - 1, 1)}
+VECTOR_RESIDUAL = {t for t in range(TILES) if t % 3 == 1}
+
+LOAD_AHEAD = 11
 
 TANH_GAIN = 1.5927812698663606
 INV_SQRT2 = 1.0 / math.sqrt(2.0)
@@ -35,96 +42,115 @@ FLOPS = 2 * (ELECTRONS + ELECTRONS // NSPIN) * 1024 * D_ONE
 
 def tile_fermilayer_pa_kernel(tc, h_one, h_two_same, h_two_diff, W1, b1, Wg, out):
     nc = tc.nc
+    pair_dram = (h_two_same, h_two_diff)
     with ExitStack() as ctx:
         ctx.enter_context(tc.manual_schedule())
         const = ctx.enter_context(tc.tile_pool(name="const", bufs=1))
+        units = ctx.enter_context(tc.tile_pool(name="units", bufs=2 * (LOAD_AHEAD + 1)))
+        h_pool = ctx.enter_context(tc.tile_pool(name="h_pool", bufs=TILES // PAIR_SETS))
+        hset_pool = ctx.enter_context(tc.tile_pool(name="hset_pool", bufs=TILES // H_SET))
         w_stage = ctx.enter_context(tc.tile_pool(name="w_stage", bufs=2))
-        h_pool = ctx.enter_context(tc.tile_pool(name="h_pool", bufs=TILES))
-        units = ctx.enter_context(tc.tile_pool(name="units", bufs=2 * (LOAD_AHEAD + 2)))
         sums = ctx.enter_context(tc.tile_pool(name="sums", bufs=2))
-        grouped_pool = ctx.enter_context(tc.tile_pool(name="grouped_pool", bufs=QUANT_LAG + 2))
-        codes_pool = ctx.enter_context(tc.tile_pool(name="codes_pool", bufs=2))
-        z_pool = ctx.enter_context(tc.tile_pool(name="z_pool", bufs=2))
-        out_pool = ctx.enter_context(tc.tile_pool(name="out_pool", bufs=6))
+        small = ctx.enter_context(tc.tile_pool(name="small", bufs=3))
+        wide = ctx.enter_context(tc.tile_pool(name="wide", bufs=4))
         psum_t = ctx.enter_context(tc.psum_pool(name="psum_t", bufs=2))
-        psum_g = ctx.enter_context(tc.psum_pool(name="psum_g", bufs=1))
         psum_pair = ctx.enter_context(tc.psum_pool(name="psum_pair", bufs=2))
-        psum_acc = ctx.enter_context(tc.psum_pool(name="psum_acc", bufs=3))
+        psum_acc = ctx.enter_context(tc.psum_pool(name="psum_acc", bufs=2))
+        psum_out = ctx.enter_context(tc.psum_pool(name="psum_out", bufs=2))
 
-        h_tiles = {}
-        same_rows = {}
-        diff_rows = {}
-        grouped_tiles = {}
+        h_tiles = []
+        pair_units = {}
+        sum_tiles = {}
+        pooled_tiles = {}
+        pair_grouped = {}
+        pair_codes = {}
         acc_tiles = {}
         z_tiles = {}
-        result_tiles = {}
+        hs_tiles = {}
+        back_tiles = {}
+        result_tiles = []
 
-        def load_tile(t):
-            h_nat = h_pool.tile([P, D_ONE], BF16, name="h_nat")
-            nc.sync.dma_start(out=h_nat[:], in_=h_one[P * t : P * (t + 1), :])
-            diff = units.tile([P, NSPIN, D_TWO], BF16, name="diff", tag="unit")
-            nc.sync.dma_start(
-                out=diff[:],
-                in_=h_two_diff[UNIT_ROWS * t : UNIT_ROWS * (t + 1), :].rearrange(
-                    "(p j) f -> p j f", j=NSPIN
-                ),
-            )
-            same = units.tile([P, NSPIN, D_TWO], BF16, name="same", tag="unit")
-            nc.sync.dma_start(
-                out=same[:],
-                in_=h_two_same[UNIT_ROWS * t : UNIT_ROWS * (t + 1), :].rearrange(
-                    "(r p) f -> p r f", p=P
-                ),
-            )
-            h_tiles[t] = h_nat
-            diff_rows[t] = diff
-            same_rows[t] = same
+        def load_pairs(t):
+            for stream in range(2):
+                unit = units.tile([P, NSPIN * D_TWO], BF16, name="unit", tag="unit")
+                rows = pair_dram[stream][TILE_ROWS * t : TILE_ROWS * (t + 1), :]
+                if (t, stream) in MATMUL_UNITS:
+                    nc.sync.dma_start(
+                        out=unit[:].rearrange("p (c x) -> p c x", c=CHUNKS),
+                        in_=rows.rearrange("(c p l) f -> p c (l f)", p=P, l=CHUNK_ROWS),
+                    )
+                else:
+                    nc.sync.dma_start(out=unit[:], in_=rows.rearrange("(p j) f -> p (j f)", j=NSPIN))
+                pair_units[t, stream] = unit
 
-        b_row = const.tile([P, D_ONE], BF16, name="b_row")
-        nc.vector.memset(b_row[:], 0.0)
-        nc.sync.dma_start(out=b_row[0:1, :], in_=b1.rearrange("(r c) -> r c", r=1))
+        b_rows = const.tile([P, P], BF16, name="b_rows")
+        nc.vector.memset(b_rows[:], 0.0)
+        nc.sync.dma_start(out=b_rows[0:PACK, :], in_=b1.rearrange("(r c) -> r c", r=PACK))
         w_raw = []
-        for w_dram in (W1, Wg):
-            raw = w_stage.tile([P, 2 * PACK, D_ONE], BF16, name="w_raw")
-            nc.sync.dma_start(out=raw[:], in_=w_dram.rearrange("(c p) f -> p c f", p=P))
-            w_raw.append(raw)
-        for t in range(LOAD_AHEAD):
-            load_tile(t)
 
+        def load_weights(w_dram):
+            raw = wide.tile([P, 2 * PACK, D_ONE], BF16, name="w_raw", tag="wide")
+            for half in range(2):
+                nc.sync.dma_start(
+                    out=raw[:, PACK * half : PACK * (half + 1), :],
+                    in_=w_dram[D_ONE * half : D_ONE * (half + 1), :].rearrange("(c p) f -> p c f", p=P),
+                )
+            w_raw.append(raw)
+
+        def load_h(b):
+            h_nat = h_pool.tile([P, PAIR_SETS, D_ONE], BF16, name="h_nat")
+            rows = h_one[PAIR_SETS * P * b : PAIR_SETS * P * (b + 1), :]
+            nc.sync.dma_start(out=h_nat[:], in_=rows.rearrange("(q p) f -> p q f", p=P))
+            for q in range(PAIR_SETS):
+                h_tiles.append(h_nat[:, q, :])
+
+        load_weights(W1)
+        for b in range(TILES // PAIR_SETS):
+            load_h(b)
+        load_weights(Wg)
+        for t in range(LOAD_AHEAD):
+            load_pairs(t)
+
+        warm = const.tile([P, 1], F32, name="warm")
+        nc.vector.memset(warm[:], 0.0)
+        nc.scalar.activation(out=warm[:], in_=warm[:], func=ACT.Tanh)
         ident_bf = const.tile([P, P], BF16, name="ident_bf")
         make_identity(nc, ident_bf[:])
         ident_f32 = const.tile([P, P], F32, name="ident_f32")
         make_identity(nc, ident_f32[:])
-        pool_f32 = const.tile([P, TILE_GROUPS], F32, name="pool_f32")
-        nc.vector.tensor_reduce(
-            out=pool_f32[:],
-            in_=ident_f32[:].rearrange("p (c i) -> p c i", i=NSPIN),
-            axis=mybir.AxisListType.X,
-            op=ADD,
-        )
-        pool_rows = const.tile([P, TILE_GROUPS], BF16, name="pool_rows")
-        nc.vector.tensor_copy(out=pool_rows[:], in_=pool_f32[:])
+        pools = {}
+        for n in (NSPIN // CHUNK_ROWS, NSPIN):
+            sums_f32 = const.tile([P, P // n], F32, name="sums_f32", tag=str(n))
+            nc.vector.tensor_reduce(
+                out=sums_f32[:],
+                in_=ident_f32[:].rearrange("p (c i) -> p c i", i=n),
+                axis=mybir.AxisListType.X,
+                op=ADD,
+            )
+            pools[n] = const.tile([P, P // n], BF16, name="pool_bf", tag="pool" + str(n))
+            nc.vector.tensor_copy(out=pools[n][:], in_=sums_f32[:])
 
-        ones = const.tile([P, P], BF16, name="ones")
-        nc.vector.memset(ones[:], 1.0)
-        b_rep_ps = psum_acc.tile([P, D_ONE], F32, name="b_rep_ps", tag="acc")
-        nc.tensor.matmul(out=b_rep_ps[:], lhsT=ones[:], rhs=b_row[:], start=True, stop=True)
-        b1_rep = const.tile([P, D_ONE], F32, name="b1_rep")
-        nc.vector.tensor_copy(out=b1_rep[:], in_=b_rep_ps[:])
+        w_codes = const.tile([P, 4, D_ONE], U32, name="w_codes", align_bytes=64)
+        w_scales = const.tile([P, 4, D_ONE], U8, name="w_scales", align_bytes=64)
 
-        w_codes = const.tile([P, PASSES, D_ONE], U32, name="w_codes", align_bytes=64)
-        w_scales = const.tile([P, PASSES, D_ONE], U8, name="w_scales", align_bytes=64)
-        for w_index in range(2):
+        w_grouped_tiles = {}
+
+        def group_weights(w_index):
             grouped = []
             for half in range(2):
                 w_grouped = w_stage.tile([P, D_ONE, PACK], BF16, name="w_grouped", align_bytes=64)
-                nc.vector.tensor_copy(
+                copy = nc.vector.tensor_copy
+                copy(
                     out=w_grouped[:].rearrange("p (c i) t -> p c t i", i=4),
                     in_=w_raw[w_index][:, PACK * half : PACK * (half + 1), :].rearrange(
                         "p t (c i) -> p c t i", i=4
                     ),
                 )
                 grouped.append(w_grouped)
+            w_grouped_tiles[w_index] = grouped
+
+        def quantise_weights(w_index):
+            grouped = w_grouped_tiles[w_index]
             for half in range(2):
                 nc.vector.quantize_mx(
                     out=w_codes[:, 2 * w_index + half, :].bitcast(FP8X4),
@@ -132,127 +158,280 @@ def tile_fermilayer_pa_kernel(tc, h_one, h_two_same, h_two_diff, W1, b1, Wg, out
                     in_=grouped[half][:].rearrange("p f t -> p (f t)"),
                 )
 
-        def sum_and_transpose(t):
-            h_nat = h_tiles[t]
-            same = same_rows[t]
-            diff = diff_rows[t]
-            grouped = grouped_pool.tile([P, PASSES, P, PACK], BF16, name="grouped", align_bytes=64)
-            grouped_tiles[t] = grouped
+        h_grouped = []
+        g_sums = []
+        h_codes = []
+        h_scales = []
+        g_own = const.tile([P, GROUPS, PACK], BF16, name="g_own", align_bytes=64)
+        g_partner = const.tile([P, GROUPS, PACK], BF16, name="g_partner", align_bytes=64)
 
-            hT = psum_t.tile([P, PACK, P], BF16, name="hT")
+        def transpose_h(t):
+            h_nat = h_tiles[t]
+            if t % H_SET == 0:
+                h_grouped.append(
+                    hset_pool.tile([P, H_SET, P, PACK], BF16, name="h_grouped", align_bytes=64)
+                )
+            hT = psum_t.tile([P, PACK, P], BF16, name="hT", tag="hT")
             for k in range(PACK):
                 nc.tensor.transpose(hT[:, k, :], h_nat[:, P * k : P * (k + 1)], ident_bf[:])
-            g_sum = psum_g.tile([P, PACK, TILE_GROUPS], F32, name="g_sum")
+            if t % H_SET == 0:
+                g_sums.append(psum_out.tile([P, PACK, H_SET * TILE_GROUPS], F32, name="g_sum", tag="back"))
             for k in range(PACK):
+                first = TILE_GROUPS * (t % H_SET)
                 nc.tensor.matmul(
-                    out=g_sum[:, k, :],
+                    out=g_sums[-1][:, k, first : first + TILE_GROUPS],
                     lhsT=h_nat[:, P * k : P * (k + 1)],
-                    rhs=pool_rows[:],
+                    rhs=pools[NSPIN][:],
                     start=True,
                     stop=True,
                 )
-            pooled = psum_pair.tile([P, PACK, P], F32, name="pooled")
-            for r in range(NSPIN):
-                for fh in range(2):
-                    nc.tensor.matmul(
-                        out=pooled[:, fh, TILE_GROUPS * r : TILE_GROUPS * (r + 1)],
-                        lhsT=same[:, r, P * fh : P * (fh + 1)],
-                        rhs=pool_rows[:],
-                        start=True,
-                        stop=True,
-                    )
-
-            sum4 = sums.tile([P, 4, D_TWO], F32, name="sum4")
-            nc.vector.tensor_tensor(out=sum4[:], in0=diff[:, 0:4, :], in1=diff[:, 4:8, :], op=ADD)
-
-            nc.scalar.copy(out=grouped[:, 0, :, :], in_=hT[:].rearrange("p k e -> p e k"))
-            by_group = g_sum[:].rearrange("p k g -> p g k")
-            nc.scalar.mul(
-                out=grouped[:, 2, :, :].rearrange("p (g i) k -> p g i k", i=NSPIN),
-                in_=by_group.unsqueeze(2).to_broadcast([P, TILE_GROUPS, NSPIN, PACK]),
-                mul=1.0 / NSPIN,
+            nc.scalar.copy(
+                out=h_grouped[-1][:, t % H_SET, :, :],
+                in_=hT[:].rearrange("p k e -> p e k"),
             )
-            partner_out = grouped[:, 3, :, :].rearrange("p (m s i) k -> p m s i k", s=2, i=NSPIN)
-            by_spin = g_sum[:].rearrange("p k (m s) -> p m s k", s=2)
-            for s in range(2):
+            if t % H_SET == H_SET - 1:
+                s = t // H_SET
                 nc.scalar.mul(
-                    out=partner_out[:, :, 1 - s, :, :],
-                    in_=by_spin[:, :, s, :]
-                    .unsqueeze(2)
-                    .to_broadcast([P, TILE_GROUPS // 2, NSPIN, PACK]),
+                    out=g_own[:, H_SET * TILE_GROUPS * s : H_SET * TILE_GROUPS * (s + 1), :],
+                    in_=g_sums[-1][:].rearrange("p k g -> p g k"),
                     mul=1.0 / NSPIN,
                 )
 
-            for fh in range(2):
-                for j in range(4):
-                    nc.tensor.matmul(
-                        out=pooled[:, 2 + fh, :],
-                        lhsT=sum4[:, j, P * fh : P * (fh + 1)],
-                        rhs=ident_f32[:],
-                        start=(j == 0),
-                        stop=(j == 3),
-                        is_transpose=True,
-                    )
-            nc.scalar.mul(
-                out=grouped[:, 1, :, :], in_=pooled[:].rearrange("p k e -> p e k"), mul=1.0 / NSPIN
-            )
-
-        def quantise_and_multiply(t):
-            grouped = grouped_tiles[t]
-            codes = codes_pool.tile([P, PASSES, P], U32, name="codes", align_bytes=64)
-            scales = codes_pool.tile([P, PASSES, P], U8, name="scales", align_bytes=64)
+        def quantise_h(s):
+            codes = hset_pool.tile([P, H_SET, P], U32, name="h_codes", align_bytes=64)
+            scales = hset_pool.tile([P, H_SET, P], U8, name="h_scales", align_bytes=64)
             nc.vector.quantize_mx(
                 out=codes[:].rearrange("p c e -> p (c e)").bitcast(FP8X4),
                 scales=scales[:].rearrange("p c e -> p (c e)"),
-                in_=grouped[:].rearrange("p c e k -> p (c e k)"),
+                in_=h_grouped[s][:].rearrange("p c e k -> p (c e k)"),
             )
-            acc = psum_acc.tile([P, D_ONE], F32, name="acc", tag="acc")
-            acc_tiles[t] = acc
-            for c in range(PASSES):
-                nc.tensor.matmul_mx(
-                    out=acc[:],
-                    lhsT=codes[:, c, :].bitcast(FP8X4),
-                    lhsT_scale=scales[:, c, :],
-                    rhs=w_codes[:, c, :].bitcast(FP8X4),
-                    rhs_scale=w_scales[:, c, :],
-                    start=(c == 0),
-                    stop=(c == PASSES - 1),
+            h_codes.append(codes)
+            h_scales.append(scales)
+
+        g_codes = const.tile([P, 2, GROUPS], U32, name="g_codes", align_bytes=64)
+        g_scales = const.tile([P, 2, GROUPS], U8, name="g_scales", align_bytes=64)
+
+        def quantise_groups():
+            by_spin = g_own[:].rearrange("p (m s) k -> p m s k", s=2)
+            partner_by_spin = g_partner[:].rearrange("p (m s) k -> p m s k", s=2)
+            for s in range(2):
+                nc.vector.tensor_copy(out=partner_by_spin[:, :, 1 - s, :], in_=by_spin[:, :, s, :])
+            for i, g_tile in enumerate((g_own, g_partner)):
+                nc.vector.quantize_mx(
+                    out=g_codes[:, i, :].bitcast(FP8X4),
+                    scales=g_scales[:, i, :],
+                    in_=g_tile[:].rearrange("p g k -> p (g k)"),
                 )
 
-        def bias_and_tanh(t):
-            z = z_pool.tile([P, D_ONE], F32, name="z")
-            z_tiles[t] = z
-            nc.vector.tensor_tensor(out=z[:], in0=acc_tiles[t][:], in1=b1_rep[:], op=ADD)
-            nc.scalar.activation(
-                out=z[:], in_=z[:], func=mybir.ActivationFunctionType.Tanh, scale=INV_SQRT2
-            )
-            result = out_pool.tile([P, D_ONE], F32, name="result")
-            result_tiles[t] = result
-            nc.scalar.mul(out=result[:], in_=h_tiles[t][:], mul=INV_SQRT2)
+        b_ps = psum_t.tile([P, P], BF16, name="b_ps", tag="hT")
+        nc.tensor.transpose(b_ps[:], b_rows[:], ident_bf[:])
+        b_cols = const.tile([P, PACK], F32, name="b_cols")
+        nc.scalar.copy(out=b_cols[:], in_=b_ps[:, 0:PACK])
 
-        def residual_and_store(t):
-            result = result_tiles[t]
-            nc.vector.scalar_tensor_tensor(
-                out=result[:],
-                in0=z_tiles[t][:],
-                scalar=TANH_GAIN * INV_SQRT2,
-                in1=result[:],
-                op0=MULT,
-                op1=ADD,
+        cb = const.tile([P, PACK, GROUPS], F32, name="cb")
+
+        def group_product():
+            for half in range(2):
+                acc = psum_acc.tile([P, 2, GROUPS], F32, name="acc_g", tag="acc")
+                for i in range(2):
+                    m = 2 * half + i
+                    for w_pass in range(2):
+                        nc.tensor.matmul_mx(
+                            out=acc[:, i, :],
+                            lhsT=w_codes[:, 2 + w_pass, P * m : P * (m + 1)].bitcast(FP8X4),
+                            lhsT_scale=w_scales[:, 2 + w_pass, P * m : P * (m + 1)],
+                            rhs=g_codes[:, w_pass, :].bitcast(FP8X4),
+                            rhs_scale=g_scales[:, w_pass, :],
+                            start=(w_pass == 0),
+                            stop=(w_pass == 1),
+                        )
+                for i in range(2):
+                    m = 2 * half + i
+                    nc.scalar.activation(
+                        out=cb[:, m, :],
+                        in_=acc[:, i, :],
+                        func=ACT.Identity,
+                        bias=b_cols[:, m : m + 1],
+                        scale=1.0,
+                    )
+
+        def add_rows(t, stream):
+            if (t, stream) in MATMUL_UNITS:
+                return
+            rows = pair_units[t, stream][:].rearrange("p (j f) -> p j f", j=NSPIN)
+            sum4 = sums.tile([P, 4, D_TWO], F32, name="sum4", tag=("same4", "diff4")[stream])
+            nc.vector.tensor_tensor(out=sum4[:], in0=rows[:, 0:4, :], in1=rows[:, 4:8, :], op=ADD)
+            sum_tiles[t, stream] = sum4
+
+        def pool_pairs(t):
+            pooled = psum_pair.tile([P, PACK, P], F32, name="pooled")
+            pooled_tiles[t] = pooled
+            for stream in range(2):
+                if (t, stream) in MATMUL_UNITS:
+                    chunks = pair_units[t, stream][:].rearrange(
+                        "p (c l f) -> p c l f", c=CHUNKS, l=CHUNK_ROWS
+                    )
+                    for c in range(CHUNKS):
+                        for fh in range(2):
+                            for l in range(CHUNK_ROWS):
+                                nc.tensor.matmul(
+                                    out=pooled[:, 2 * stream + fh, CHUNK_COLS * c : CHUNK_COLS * (c + 1)],
+                                    lhsT=chunks[:, c, l, P * fh : P * (fh + 1)],
+                                    rhs=pools[NSPIN // CHUNK_ROWS][:],
+                                    start=(l == 0),
+                                    stop=(l == CHUNK_ROWS - 1),
+                                )
+                else:
+                    sum4 = sum_tiles[t, stream]
+                    for fh in range(2):
+                        for j in range(4):
+                            nc.tensor.matmul(
+                                out=pooled[:, 2 * stream + fh, :],
+                                lhsT=sum4[:, j, P * fh : P * (fh + 1)],
+                                rhs=ident_f32[:],
+                                start=(j == 0),
+                                stop=(j == 3),
+                                is_transpose=True,
+                            )
+
+        def group_pairs(t):
+            grouped = small.tile([P, P, PACK], BF16, name="grouped", align_bytes=64)
+            pair_grouped[t] = grouped
+            nc.scalar.mul(
+                out=grouped[:], in_=pooled_tiles[t][:].rearrange("p k e -> p e k"), mul=1.0 / NSPIN
             )
-            nc.sync.dma_start(out=out[P * t : P * (t + 1), :], in_=result[:])
+
+        def quantise_pairs(t):
+            codes = small.tile([P, P], U32, name="codes", align_bytes=64)
+            scales = small.tile([P, P], U8, name="scales", align_bytes=64)
+            nc.vector.quantize_mx(
+                out=codes[:].bitcast(FP8X4),
+                scales=scales[:],
+                in_=pair_grouped[t][:].rearrange("p e k -> p (e k)"),
+            )
+            pair_codes[t] = (codes, scales)
+
+        def multiply(t):
+            s, i = divmod(t, H_SET)
+            moving = (
+                (h_codes[s][:, i, :], h_scales[s][:, i, :]),
+                (pair_codes[t][0][:], pair_codes[t][1][:]),
+            )
+            acc = psum_acc.tile([P, PACK, P], F32, name="acc", tag="acc")
+            acc_tiles[t] = acc
+            for m in range(PACK):
+                for w_pass in range(2):
+                    nc.tensor.matmul_mx(
+                        out=acc[:, m, :],
+                        lhsT=w_codes[:, w_pass, P * m : P * (m + 1)].bitcast(FP8X4),
+                        lhsT_scale=w_scales[:, w_pass, P * m : P * (m + 1)],
+                        rhs=moving[w_pass][0].bitcast(FP8X4),
+                        rhs_scale=moving[w_pass][1],
+                        start=(w_pass == 0),
+                        stop=(w_pass == 1),
+                    )
+
+        def add_group_term(t):
+            z = small.tile([P, PACK, P], F32, name="z")
+            z_tiles[t] = z
+            term = cb[:, :, TILE_GROUPS * t : TILE_GROUPS * (t + 1)]
+            nc.vector.tensor_tensor(
+                out=z[:].rearrange("p m (g i) -> p m g i", i=NSPIN),
+                in0=acc_tiles[t][:].rearrange("p m (g i) -> p m g i", i=NSPIN),
+                in1=term.unsqueeze(3).to_broadcast([P, PACK, TILE_GROUPS, NSPIN]),
+                op=ADD,
+            )
+
+        def tanh(t):
+            z = z_tiles[t]
+            nc.scalar.activation(out=z[:], in_=z[:], func=ACT.Tanh, scale=INV_SQRT2)
+
+        def h_by_feature(t):
+            s, i = divmod(t, H_SET)
+            return h_grouped[s][:, i, :, :].rearrange("p e k -> p k e")
+
+        def scale_h(t):
+            if t in VECTOR_RESIDUAL:
+                return
+            hs = small.tile([P, PACK, P], F32, name="hs")
+            hs_tiles[t] = hs
+            nc.scalar.mul(out=hs[:], in_=h_by_feature(t), mul=1.0 / TANH_GAIN)
+
+        def add_residual(t):
+            if t not in VECTOR_RESIDUAL:
+                return
+            z = z_tiles[t]
+            nc.vector.scalar_tensor_tensor(
+                out=z[:], in0=z[:], scalar=TANH_GAIN, in1=h_by_feature(t), op0=MULT, op1=ADD
+            )
+
+        def transpose_back(t):
+            back = psum_out.tile([P, PACK, P], F32, name="back", tag="back")
+            back_tiles[t] = back
+            parts = (z_tiles[t],) if t in VECTOR_RESIDUAL else (hs_tiles[t], z_tiles[t])
+            for m in range(PACK):
+                for i, part in enumerate(parts):
+                    nc.tensor.matmul(
+                        out=back[:, m, :],
+                        lhsT=part[:, m, :],
+                        rhs=ident_f32[:],
+                        start=(i == 0),
+                        stop=(i == len(parts) - 1),
+                        is_transpose=True,
+                    )
+
+        def store(t):
+            if t % H_SET == 0:
+                result_tiles.append(wide.tile([P, H_SET, D_ONE], F32, name="result", tag="wide"))
+            i = t % H_SET
+            nc.scalar.mul(
+                out=result_tiles[-1][:, i, :],
+                in_=back_tiles[t][:].rearrange("p m f -> p (m f)"),
+                mul=INV_SQRT2 if t in VECTOR_RESIDUAL else TANH_GAIN * INV_SQRT2,
+            )
+            n = 1 if t >= TILES - 2 else 2
+            if t % n == n - 1:
+                first = t - n + 1
+                nc.sync.dma_start(
+                    out=out[P * first : P * (t + 1), :].rearrange("(q p) f -> p q f", p=P),
+                    in_=result_tiles[-1][:, i - n + 1 : i + 1, :],
+                )
 
         def is_tile(t):
             return 0 <= t < TILES
 
-        for i in range(TILES + FINISH_LAG):
-            if is_tile(i + LOAD_AHEAD):
-                load_tile(i + LOAD_AHEAD)
-            if is_tile(i - FINISH_LAG):
-                bias_and_tanh(i - FINISH_LAG)
-            if is_tile(i):
-                sum_and_transpose(i)
-            if is_tile(i - QUANT_LAG):
-                quantise_and_multiply(i - QUANT_LAG)
-            if is_tile(i - FINISH_LAG):
-                residual_and_store(i - FINISH_LAG)
+        group_weights(0)
+        for t in range(TILES):
+            transpose_h(t)
+        quantise_weights(0)
+        for i in range(TILES // H_SET):
+            quantise_h(i)
+        group_weights(1)
+        quantise_groups()
+        quantise_weights(1)
+        for r in range(TILES + 5):
+            if is_tile(r - 4):
+                add_group_term(r - 4)
+                tanh(r - 4)
+            if is_tile(r - 5):
+                add_residual(r - 5)
+            if is_tile(r):
+                add_rows(r, 0)
+                add_rows(r, 1)
+            if is_tile(r - 2):
+                quantise_pairs(r - 2)
+            if is_tile(r - 3):
+                multiply(r - 3)
+                scale_h(r - 3)
+            if is_tile(r - 5):
+                transpose_back(r - 5)
+            if r == 1:
+                group_product()
+            if is_tile(r - 5):
+                store(r - 5)
+            if is_tile(r):
+                pool_pairs(r)
+            if is_tile(r - 1):
+                group_pairs(r - 1)
+            if r + LOAD_AHEAD < TILES:
+                load_pairs(r + LOAD_AHEAD)

@@ -44,7 +44,6 @@ def tile_fermilayer_pa_kernel(tc, h_one, h_two_same, h_two_diff, W1, b1, Wg, out
     nc = tc.nc
     pair_dram = (h_two_same, h_two_diff)
     with ExitStack() as ctx:
-        ctx.enter_context(tc.manual_schedule())
         const = ctx.enter_context(tc.tile_pool(name="const", bufs=1))
         units = ctx.enter_context(tc.tile_pool(name="units", bufs=2 * (LOAD_AHEAD + 1)))
         h_pool = ctx.enter_context(tc.tile_pool(name="h_pool", bufs=TILES // PAIR_SETS))

@@ -29,8 +29,8 @@ CHUNK_COLS = P // CHUNKS
 H_SET = 4
 PAIR_SETS = 2
 
-MATMUL_UNITS = {(t, 0) for t in range(TILES) if t % 3 != 1} | {(TILES - 1, 1)}
-VECTOR_RESIDUAL = {t for t in range(TILES) if t % 3 == 1}
+MATMUL_UNITS = {(t, 1) for t in range(TILES) if t % 4 != 3}
+VECTOR_RESIDUAL = {t for t in range(TILES) if True}
 
 LOAD_AHEAD = 11
 
@@ -138,7 +138,7 @@ def tile_fermilayer_pa_kernel(tc, h_one, h_two_same, h_two_diff, W1, b1, Wg, out
             grouped = []
             for half in range(2):
                 w_grouped = w_stage.tile([P, D_ONE, PACK], BF16, name="w_grouped", align_bytes=64)
-                copy = nc.vector.tensor_copy
+                copy = nc.vector.tensor_copy if w_index == 0 else nc.scalar.copy
                 copy(
                     out=w_grouped[:].rearrange("p (c i) t -> p c t i", i=4),
                     in_=w_raw[w_index][:, PACK * half : PACK * (half + 1), :].rearrange(
@@ -318,6 +318,16 @@ def tile_fermilayer_pa_kernel(tc, h_one, h_two_same, h_two_diff, W1, b1, Wg, out
             )
             acc = psum_acc.tile([P, PACK, P], F32, name="acc", tag="acc")
             acc_tiles[t] = acc
+            for i in range(2):
+                nc.tensor.matmul_mx(
+                    out=acc[:, i % PACK, :],
+                    lhsT=w_codes[:, 1, P * (i % PACK) : P * (i % PACK + 1)].bitcast(FP8X4),
+                    lhsT_scale=w_scales[:, 1, P * (i % PACK) : P * (i % PACK + 1)],
+                    rhs=moving[1][0].bitcast(FP8X4),
+                    rhs_scale=moving[1][1],
+                    start=True,
+                    stop=True,
+                )
             for m in range(PACK):
                 for w_pass in range(2):
                     nc.tensor.matmul_mx(

@@ -29,8 +29,7 @@ CHUNK_COLS = P // CHUNKS
 H_SET = 4
 PAIR_SETS = 2
 
-MATMUL_UNITS = {(t, 1) for t in range(TILES) if t % 4 != 3}
-VECTOR_RESIDUAL = {t for t in range(TILES) if True}
+MATMUL_UNITS = {(t, 1) for t in range(4, TILES)}
 
 LOAD_AHEAD = 11
 
@@ -65,7 +64,6 @@ def tile_fermilayer_pa_kernel(tc, h_one, h_two_same, h_two_diff, W1, b1, Wg, out
         pair_codes = {}
         acc_tiles = {}
         z_tiles = {}
-        hs_tiles = {}
         back_tiles = {}
         result_tiles = []
 
@@ -82,18 +80,23 @@ def tile_fermilayer_pa_kernel(tc, h_one, h_two_same, h_two_diff, W1, b1, Wg, out
                     nc.sync.dma_start(out=unit[:], in_=rows.rearrange("(p j) f -> p (j f)", j=NSPIN))
                 pair_units[t, stream] = unit
 
-        b_rows = const.tile([P, P], BF16, name="b_rows")
+        b_rows = const.tile([P, 2 * P], BF16, name="b_rows")
         nc.vector.memset(b_rows[:], 0.0)
-        nc.sync.dma_start(out=b_rows[0:PACK, :], in_=b1.rearrange("(r c) -> r c", r=PACK))
+        nc.sync.dma_start(out=b_rows[0:2, :], in_=b1.rearrange("(u x) -> u x", u=2))
         w_raw = []
 
         def load_weights(w_dram):
             raw = wide.tile([P, 2 * PACK, D_ONE], BF16, name="w_raw", tag="wide")
             for half in range(2):
-                nc.sync.dma_start(
-                    out=raw[:, PACK * half : PACK * (half + 1), :],
-                    in_=w_dram[D_ONE * half : D_ONE * (half + 1), :].rearrange("(c p) f -> p c f", p=P),
-                )
+                rows = w_dram[D_ONE * half : D_ONE * (half + 1), :]
+                tile_rows = raw[:, PACK * half : PACK * (half + 1), :]
+                if w_dram is W1 and half == 0:
+                    nc.sync.dma_start(
+                        out=tile_rows.rearrange("p (u e) f -> p u (e f)", u=2),
+                        in_=rows.rearrange("(u p e) f -> p u (e f)", u=2, e=2),
+                    )
+                else:
+                    nc.sync.dma_start(out=tile_rows, in_=rows.rearrange("(c p) f -> p c f", p=P))
             w_raw.append(raw)
 
         def load_h(b):
@@ -103,11 +106,12 @@ def tile_fermilayer_pa_kernel(tc, h_one, h_two_same, h_two_diff, W1, b1, Wg, out
             for q in range(PAIR_SETS):
                 h_tiles.append(h_nat[:, q, :])
 
+        load_pairs(0)
         load_weights(W1)
         for b in range(TILES // PAIR_SETS):
             load_h(b)
         load_weights(Wg)
-        for t in range(LOAD_AHEAD):
+        for t in range(1, LOAD_AHEAD):
             load_pairs(t)
 
         warm = const.tile([P, 1], F32, name="warm")
@@ -139,12 +143,15 @@ def tile_fermilayer_pa_kernel(tc, h_one, h_two_same, h_two_diff, W1, b1, Wg, out
             for half in range(2):
                 w_grouped = w_stage.tile([P, D_ONE, PACK], BF16, name="w_grouped", align_bytes=64)
                 copy = nc.vector.tensor_copy if w_index == 0 else nc.scalar.copy
-                copy(
-                    out=w_grouped[:].rearrange("p (c i) t -> p c t i", i=4),
-                    in_=w_raw[w_index][:, PACK * half : PACK * (half + 1), :].rearrange(
-                        "p t (c i) -> p c t i", i=4
-                    ),
+                by_feature = w_raw[w_index][:, PACK * half : PACK * (half + 1), :].rearrange(
+                    "p t (u q e) -> p t u q e", u=2, e=2
                 )
+                for m in range(PACK):
+                    u, e = divmod(m, 2)
+                    copy(
+                        out=w_grouped[:, P * m : P * (m + 1), :].rearrange("p (c i) t -> p c t i", i=4),
+                        in_=by_feature[:, :, u, :, e].rearrange("p t (c i) -> p c t i", i=4),
+                    )
                 grouped.append(w_grouped)
             w_grouped_tiles[w_index] = grouped
 
@@ -170,9 +177,10 @@ def tile_fermilayer_pa_kernel(tc, h_one, h_two_same, h_two_diff, W1, b1, Wg, out
                 h_grouped.append(
                     hset_pool.tile([P, H_SET, P, PACK], BF16, name="h_grouped", align_bytes=64)
                 )
-            hT = psum_t.tile([P, PACK, P], BF16, name="hT", tag="hT")
-            for k in range(PACK):
-                nc.tensor.transpose(hT[:, k, :], h_nat[:, P * k : P * (k + 1)], ident_bf[:])
+            hT = psum_t.tile([P, 2, P], F32, name="hT", tag="hT")
+            words = h_nat.bitcast(F32)
+            for u in range(2):
+                nc.tensor.transpose(hT[:, u, :], words[:, P * u : P * (u + 1)], ident_f32[:])
             if t % H_SET == 0:
                 g_sums.append(psum_out.tile([P, PACK, H_SET * TILE_GROUPS], F32, name="g_sum", tag="back"))
             for k in range(PACK):
@@ -185,8 +193,11 @@ def tile_fermilayer_pa_kernel(tc, h_one, h_two_same, h_two_diff, W1, b1, Wg, out
                     stop=True,
                 )
             nc.scalar.copy(
-                out=h_grouped[-1][:, t % H_SET, :, :],
-                in_=hT[:].rearrange("p k e -> p e k"),
+                out=h_grouped[-1][:, t % H_SET, :, :]
+                .rearrange("p e k -> p (e k)")
+                .bitcast(F32)
+                .rearrange("p (e u) -> p e u", u=2),
+                in_=hT[:].rearrange("p u e -> p e u"),
             )
             if t % H_SET == H_SET - 1:
                 s = t // H_SET
@@ -222,10 +233,14 @@ def tile_fermilayer_pa_kernel(tc, h_one, h_two_same, h_two_diff, W1, b1, Wg, out
                     in_=g_tile[:].rearrange("p g k -> p (g k)"),
                 )
 
-        b_ps = psum_t.tile([P, P], BF16, name="b_ps", tag="hT")
-        nc.tensor.transpose(b_ps[:], b_rows[:], ident_bf[:])
+        b_ps = psum_t.tile([P, 2, P], BF16, name="b_ps", tag="hT")
+        by_parity = b_rows[:].rearrange("p (x e) -> p e x", e=2)
+        for e in range(2):
+            nc.tensor.transpose(b_ps[:, e, :], by_parity[:, e, :], ident_bf[:])
         b_cols = const.tile([P, PACK], F32, name="b_cols")
-        nc.scalar.copy(out=b_cols[:], in_=b_ps[:, 0:PACK])
+        nc.scalar.copy(
+            out=b_cols[:].rearrange("p (u e) -> p e u", e=2), in_=b_ps[:, :, 0:2]
+        )
 
         cb = const.tile([P, PACK, GROUPS], F32, name="cb")
 
@@ -318,7 +333,7 @@ def tile_fermilayer_pa_kernel(tc, h_one, h_two_same, h_two_diff, W1, b1, Wg, out
             )
             acc = psum_acc.tile([P, PACK, P], F32, name="acc", tag="acc")
             acc_tiles[t] = acc
-            for i in range(2):
+            for i in range(4):
                 nc.tensor.matmul_mx(
                     out=acc[:, i % PACK, :],
                     lhsT=w_codes[:, 1, P * (i % PACK) : P * (i % PACK + 1)].bitcast(FP8X4),
@@ -359,16 +374,7 @@ def tile_fermilayer_pa_kernel(tc, h_one, h_two_same, h_two_diff, W1, b1, Wg, out
             s, i = divmod(t, H_SET)
             return h_grouped[s][:, i, :, :].rearrange("p e k -> p k e")
 
-        def scale_h(t):
-            if t in VECTOR_RESIDUAL:
-                return
-            hs = small.tile([P, PACK, P], F32, name="hs")
-            hs_tiles[t] = hs
-            nc.scalar.mul(out=hs[:], in_=h_by_feature(t), mul=1.0 / TANH_GAIN)
-
         def add_residual(t):
-            if t not in VECTOR_RESIDUAL:
-                return
             z = z_tiles[t]
             nc.vector.scalar_tensor_tensor(
                 out=z[:], in0=z[:], scalar=TANH_GAIN, in1=h_by_feature(t), op0=MULT, op1=ADD
@@ -377,26 +383,17 @@ def tile_fermilayer_pa_kernel(tc, h_one, h_two_same, h_two_diff, W1, b1, Wg, out
         def transpose_back(t):
             back = psum_out.tile([P, PACK, P], F32, name="back", tag="back")
             back_tiles[t] = back
-            parts = (z_tiles[t],) if t in VECTOR_RESIDUAL else (hs_tiles[t], z_tiles[t])
             for m in range(PACK):
-                for i, part in enumerate(parts):
-                    nc.tensor.matmul(
-                        out=back[:, m, :],
-                        lhsT=part[:, m, :],
-                        rhs=ident_f32[:],
-                        start=(i == 0),
-                        stop=(i == len(parts) - 1),
-                        is_transpose=True,
-                    )
+                nc.tensor.transpose(back[:, m, :], z_tiles[t][:, m, :], ident_f32[:])
 
         def store(t):
             if t % H_SET == 0:
                 result_tiles.append(wide.tile([P, H_SET, D_ONE], F32, name="result", tag="wide"))
             i = t % H_SET
             nc.scalar.mul(
-                out=result_tiles[-1][:, i, :],
-                in_=back_tiles[t][:].rearrange("p m f -> p (m f)"),
-                mul=INV_SQRT2 if t in VECTOR_RESIDUAL else TANH_GAIN * INV_SQRT2,
+                out=result_tiles[-1][:, i, :].rearrange("p (u q e) -> p u q e", u=2, e=2),
+                in_=back_tiles[t][:].rearrange("p (u e) q -> p u q e", u=2),
+                mul=INV_SQRT2,
             )
             n = 1 if t >= TILES - 2 else 2
             if t % n == n - 1:
@@ -431,7 +428,6 @@ def tile_fermilayer_pa_kernel(tc, h_one, h_two_same, h_two_diff, W1, b1, Wg, out
                 quantise_pairs(r - 2)
             if is_tile(r - 3):
                 multiply(r - 3)
-                scale_h(r - 3)
             if is_tile(r - 5):
                 transpose_back(r - 5)
             if r == 1:

@@ -83,7 +83,7 @@ def tile_fermilayer_pa_kernel(tc, h_one, h_two_same, h_two_diff, W1, b1, Wg, out
         b_rows = const.tile([P, 2 * P], BF16, name="b_rows")
         nc.vector.memset(b_rows[:], 0.0)
         nc.sync.dma_start(out=b_rows[0:2, :], in_=b1.rearrange("(u x) -> u x", u=2))
-        w_raw = []
+        w_raw = {}
 
         def load_weights(w_dram):
             raw = wide.tile([P, 2 * PACK, D_ONE], BF16, name="w_raw", tag="wide")
@@ -97,7 +97,7 @@ def tile_fermilayer_pa_kernel(tc, h_one, h_two_same, h_two_diff, W1, b1, Wg, out
                     )
                 else:
                     nc.sync.dma_start(out=tile_rows, in_=rows.rearrange("(c p) f -> p c f", p=P))
-            w_raw.append(raw)
+            w_raw[w_dram is Wg] = raw
 
         def load_h(b):
             h_nat = h_pool.tile([P, PAIR_SETS, D_ONE], BF16, name="h_nat")
@@ -246,7 +246,7 @@ def tile_fermilayer_pa_kernel(tc, h_one, h_two_same, h_two_diff, W1, b1, Wg, out
 
         def group_product():
             for half in range(2):
-                acc = psum_acc.tile([P, 2, GROUPS], F32, name="acc_g", tag="acc")
+                acc = psum_t.tile([P, 2, GROUPS], F32, name="acc_g", tag="hT")
                 for i in range(2):
                     m = 2 * half + i
                     for w_pass in range(2):
@@ -333,16 +333,6 @@ def tile_fermilayer_pa_kernel(tc, h_one, h_two_same, h_two_diff, W1, b1, Wg, out
             )
             acc = psum_acc.tile([P, PACK, P], F32, name="acc", tag="acc")
             acc_tiles[t] = acc
-            for i in range(4):
-                nc.tensor.matmul_mx(
-                    out=acc[:, i % PACK, :],
-                    lhsT=w_codes[:, 1, P * (i % PACK) : P * (i % PACK + 1)].bitcast(FP8X4),
-                    lhsT_scale=w_scales[:, 1, P * (i % PACK) : P * (i % PACK + 1)],
-                    rhs=moving[1][0].bitcast(FP8X4),
-                    rhs_scale=moving[1][1],
-                    start=True,
-                    stop=True,
-                )
             for m in range(PACK):
                 for w_pass in range(2):
                     nc.tensor.matmul_mx(

@@ -31,6 +31,8 @@ PAIR_SETS = 2
 
 MATMUL_UNITS = {(t, 1) for t in range(4, TILES)}
 
+TENSOR_RESIDUAL = {t for t in range(TILES) if t % 4 == 3}
+
 LOAD_AHEAD = 11
 
 TANH_GAIN = 1.5927812698663606
@@ -65,6 +67,7 @@ def tile_fermilayer_pa_kernel(tc, h_one, h_two_same, h_two_diff, W1, b1, Wg, out
         acc_tiles = {}
         z_tiles = {}
         back_tiles = {}
+        hs_tiles = {}
         result_tiles = []
 
         def load_pairs(t):
@@ -366,15 +369,32 @@ def tile_fermilayer_pa_kernel(tc, h_one, h_two_same, h_two_diff, W1, b1, Wg, out
 
         def add_residual(t):
             z = z_tiles[t]
+            if t in TENSOR_RESIDUAL:
+                return
             nc.vector.scalar_tensor_tensor(
                 out=z[:], in0=z[:], scalar=TANH_GAIN, in1=h_by_feature(t), op0=MULT, op1=ADD
             )
 
+        def scale_h(t):
+            if t not in TENSOR_RESIDUAL:
+                return
+            hs_tiles[t] = small.tile([P, PACK, P], F32, name="hs")
+            nc.scalar.mul(out=hs_tiles[t][:], in_=h_by_feature(t), mul=1.0 / TANH_GAIN)
+
         def transpose_back(t):
             back = psum_out.tile([P, PACK, P], F32, name="back", tag="back")
             back_tiles[t] = back
+            parts = (hs_tiles[t], z_tiles[t]) if t in TENSOR_RESIDUAL else (z_tiles[t],)
             for m in range(PACK):
-                nc.tensor.transpose(back[:, m, :], z_tiles[t][:, m, :], ident_f32[:])
+                for i, part in enumerate(parts):
+                    nc.tensor.matmul(
+                        out=back[:, m, :],
+                        lhsT=part[:, m, :],
+                        rhs=ident_f32[:],
+                        start=(i == 0),
+                        stop=(i == len(parts) - 1),
+                        is_transpose=True,
+                    )
 
         def store(t):
             if t % H_SET == 0:
@@ -383,7 +403,7 @@ def tile_fermilayer_pa_kernel(tc, h_one, h_two_same, h_two_diff, W1, b1, Wg, out
             nc.scalar.mul(
                 out=result_tiles[-1][:, i, :].rearrange("p (u q e) -> p u q e", u=2, e=2),
                 in_=back_tiles[t][:].rearrange("p (u e) q -> p u q e", u=2),
-                mul=INV_SQRT2,
+                mul=TANH_GAIN * INV_SQRT2 if t in TENSOR_RESIDUAL else INV_SQRT2,
             )
             n = 1 if t >= TILES - 2 else 2
             if t % n == n - 1:
@@ -418,6 +438,7 @@ def tile_fermilayer_pa_kernel(tc, h_one, h_two_same, h_two_diff, W1, b1, Wg, out
                 quantise_pairs(r - 2)
             if is_tile(r - 3):
                 multiply(r - 3)
+                scale_h(r - 3)
             if is_tile(r - 5):
                 transpose_back(r - 5)
             if r == 1:

@@ -31,7 +31,7 @@ PAIR_SETS = 2
 
 MATMUL_UNITS = {(t, 1) for t in range(4, TILES)}
 
-TENSOR_RESIDUAL = {t for t in range(TILES) if t % 4 == 3}
+TENSOR_RESIDUAL = {t for t in range(TILES) if t % 4 == 1}
 
 LOAD_AHEAD = 11
 
@@ -405,7 +405,7 @@ def tile_fermilayer_pa_kernel(tc, h_one, h_two_same, h_two_diff, W1, b1, Wg, out
                 in_=back_tiles[t][:].rearrange("p (u e) q -> p u q e", u=2),
                 mul=TANH_GAIN * INV_SQRT2 if t in TENSOR_RESIDUAL else INV_SQRT2,
             )
-            n = 1 if t >= TILES - 2 else 2
+            n = 1 if t >= TILES - 4 else 2
             if t % n == n - 1:
                 first = t - n + 1
                 nc.sync.dma_start(

@@ -93,7 +93,7 @@ def tile_fermilayer_pa_kernel(tc, h_one, h_two_same, h_two_diff, W1, b1, Wg, out
             for half in range(2):
                 rows = w_dram[D_ONE * half : D_ONE * (half + 1), :]
                 tile_rows = raw[:, PACK * half : PACK * (half + 1), :]
-                if w_dram is W1 and half == 0:
+                if w_dram is Wg or half == 0:
                     nc.sync.dma_start(
                         out=tile_rows.rearrange("p (u e) f -> p u (e f)", u=2),
                         in_=rows.rearrange("(u p e) f -> p u (e f)", u=2, e=2),
@@ -182,6 +182,7 @@ def tile_fermilayer_pa_kernel(tc, h_one, h_two_same, h_two_diff, W1, b1, Wg, out
                 )
             hT = psum_t.tile([P, 2, P], F32, name="hT", tag="hT")
             words = h_nat.bitcast(F32)
+            by_parity = h_nat.rearrange("p (u q e) -> p u e q", u=2, e=2)
             for u in range(2):
                 nc.tensor.transpose(hT[:, u, :], words[:, P * u : P * (u + 1)], ident_f32[:])
             if t % H_SET == 0:
@@ -190,7 +191,7 @@ def tile_fermilayer_pa_kernel(tc, h_one, h_two_same, h_two_diff, W1, b1, Wg, out
                 first = TILE_GROUPS * (t % H_SET)
                 nc.tensor.matmul(
                     out=g_sums[-1][:, k, first : first + TILE_GROUPS],
-                    lhsT=h_nat[:, P * k : P * (k + 1)],
+                    lhsT=by_parity[:, k // 2, k % 2, :],
                     rhs=pools[NSPIN][:],
                     start=True,
                     stop=True,
@@ -400,17 +401,26 @@ def tile_fermilayer_pa_kernel(tc, h_one, h_two_same, h_two_diff, W1, b1, Wg, out
             if t % H_SET == 0:
                 result_tiles.append(wide.tile([P, H_SET, D_ONE], F32, name="result", tag="wide"))
             i = t % H_SET
-            nc.scalar.mul(
-                out=result_tiles[-1][:, i, :].rearrange("p (u q e) -> p u q e", u=2, e=2),
-                in_=back_tiles[t][:].rearrange("p (u e) q -> p u q e", u=2),
-                mul=TANH_GAIN * INV_SQRT2 if t in TENSOR_RESIDUAL else INV_SQRT2,
-            )
+            result = result_tiles[-1]
+            factor = TANH_GAIN * INV_SQRT2 if t in TENSOR_RESIDUAL else INV_SQRT2
+            parts = 2 if t == TILES - 1 else 1
+            width = D_ONE // parts
+            for part in range(parts):
+                columns = slice(width * part, width * (part + 1))
+                features = slice(PACK // parts * part, PACK // parts * (part + 1))
+                nc.scalar.mul(
+                    out=result[:, i, columns].rearrange("p (u q e) -> p u q e", q=P, e=2),
+                    in_=back_tiles[t][:, features, :].rearrange("p (u e) q -> p u q e", e=2),
+                    mul=factor,
+                )
+                if parts == 2:
+                    nc.sync.dma_start(out=out[P * t : P * (t + 1), columns], in_=result[:, i, columns])
             n = 1 if t >= TILES - 4 else 2
-            if t % n == n - 1:
+            if parts == 1 and t % n == n - 1:
                 first = t - n + 1
                 nc.sync.dma_start(
                     out=out[P * first : P * (t + 1), :].rearrange("(q p) f -> p q f", p=P),
-                    in_=result_tiles[-1][:, i - n + 1 : i + 1, :],
+                    in_=result[:, i - n + 1 : i + 1, :],
                 )
 
         def is_tile(t):

from contextlib import ExitStack
import math

import concourse.mybir as mybir
from concourse.masks import make_identity

F32 = mybir.dt.float32
BF16 = mybir.dt.bfloat16
U32 = mybir.dt.uint32
U8 = mybir.dt.uint8
FP8X4 = mybir.dt.float8_e4m3fn_x4
ADD = mybir.AluOpType.add
MULT = mybir.AluOpType.mult
ACT = mybir.ActivationFunctionType

P = 128
PACK = 4
NSPIN = 8
D_ONE = 512
D_TWO = 256
ELECTRONS = 2048
TILES = ELECTRONS // P
GROUPS = ELECTRONS // NSPIN
TILE_GROUPS = P // NSPIN
TILE_ROWS = P * NSPIN
CHUNK_ROWS = 2
CHUNKS = TILE_ROWS // (P * CHUNK_ROWS)
CHUNK_COLS = P // CHUNKS
H_SET = 4
PAIR_SETS = 2

MATMUL_UNITS = {(t, 1) for t in range(4, TILES)}

TENSOR_RESIDUAL = {t for t in range(TILES) if t % 4 == 1}

LOAD_AHEAD = 11

TANH_GAIN = 1.5927812698663606
INV_SQRT2 = 1.0 / math.sqrt(2.0)

FLOPS = 2 * (ELECTRONS + ELECTRONS // NSPIN) * 1024 * D_ONE


def tile_fermilayer_pa_kernel(tc, h_one, h_two_same, h_two_diff, W1, b1, Wg, out):
    nc = tc.nc
    pair_dram = (h_two_same, h_two_diff)
    with ExitStack() as ctx:
        const = ctx.enter_context(tc.tile_pool(name="const", bufs=1))
        units = ctx.enter_context(tc.tile_pool(name="units", bufs=2 * (LOAD_AHEAD + 1)))
        h_pool = ctx.enter_context(tc.tile_pool(name="h_pool", bufs=TILES // PAIR_SETS))
        hset_pool = ctx.enter_context(tc.tile_pool(name="hset_pool", bufs=TILES // H_SET))
        w_stage = ctx.enter_context(tc.tile_pool(name="w_stage", bufs=2))
        sums = ctx.enter_context(tc.tile_pool(name="sums", bufs=2))
        small = ctx.enter_context(tc.tile_pool(name="small", bufs=3))
        wide = ctx.enter_context(tc.tile_pool(name="wide", bufs=4))
        psum_t = ctx.enter_context(tc.psum_pool(name="psum_t", bufs=2))
        psum_pair = ctx.enter_context(tc.psum_pool(name="psum_pair", bufs=2))
        psum_acc = ctx.enter_context(tc.psum_pool(name="psum_acc", bufs=2))
        psum_out = ctx.enter_context(tc.psum_pool(name="psum_out", bufs=2))

        h_tiles = []
        pair_units = {}
        sum_tiles = {}
        pooled_tiles = {}
        pair_grouped = {}
        pair_codes = {}
        acc_tiles = {}
        z_tiles = {}
        back_tiles = {}
        hs_tiles = {}
        result_tiles = []

        def load_pairs(t):
            for stream in range(2):
                unit = units.tile([P, NSPIN * D_TWO], BF16, name="unit", tag="unit")
                rows = pair_dram[stream][TILE_ROWS * t : TILE_ROWS * (t + 1), :]
                if (t, stream) in MATMUL_UNITS:
                    nc.sync.dma_start(
                        out=unit[:].rearrange("p (c x) -> p c x", c=CHUNKS),
                        in_=rows.rearrange("(c p l) f -> p c (l f)", p=P, l=CHUNK_ROWS),
                    )
                else:
                    nc.sync.dma_start(out=unit[:], in_=rows.rearrange("(p j) f -> p (j f)", j=NSPIN))
                pair_units[t, stream] = unit

        b_rows = const.tile([P, 2 * P], BF16, name="b_rows")
        nc.vector.memset(b_rows[:], 0.0)
        nc.sync.dma_start(out=b_rows[0:2, :], in_=b1.rearrange("(u x) -> u x", u=2))
        w_raw = {}

        def load_weights(w_dram):
            raw = wide.tile([P, 2 * PACK, D_ONE], BF16, name="w_raw", tag="wide")
            for half in range(2):
                rows = w_dram[D_ONE * half : D_ONE * (half + 1), :]
                tile_rows = raw[:, PACK * half : PACK * (half + 1), :]
                if w_dram is Wg or half == 0:
                    nc.sync.dma_start(
                        out=tile_rows.rearrange("p (u e) f -> p u (e f)", u=2),
                        in_=rows.rearrange("(u p e) f -> p u (e f)", u=2, e=2),
                    )
                else:
                    nc.sync.dma_start(out=tile_rows, in_=rows.rearrange("(c p) f -> p c f", p=P))
            w_raw[w_dram is Wg] = raw

        def load_h(b):
            h_nat = h_pool.tile([P, PAIR_SETS, D_ONE], BF16, name="h_nat")
            rows = h_one[PAIR_SETS * P * b : PAIR_SETS * P * (b + 1), :]
            nc.sync.dma_start(out=h_nat[:], in_=rows.rearrange("(q p) f -> p q f", p=P))
            for q in range(PAIR_SETS):
                h_tiles.append(h_nat[:, q, :])

        load_pairs(0)
        load_weights(W1)
        for b in range(TILES // PAIR_SETS):
            load_h(b)
        load_weights(Wg)
        for t in range(1, LOAD_AHEAD):
            load_pairs(t)

        warm = const.tile([P, 1], F32, name="warm")
        nc.vector.memset(warm[:], 0.0)
        nc.scalar.activation(out=warm[:], in_=warm[:], func=ACT.Tanh)
        ident_bf = const.tile([P, P], BF16, name="ident_bf")
        make_identity(nc, ident_bf[:])
        ident_f32 = const.tile([P, P], F32, name="ident_f32")
        make_identity(nc, ident_f32[:])
        pools = {}
        for n in (NSPIN // CHUNK_ROWS, NSPIN):
            sums_f32 = const.tile([P, P // n], F32, name="sums_f32", tag=str(n))
            nc.vector.tensor_reduce(
                out=sums_f32[:],
                in_=ident_f32[:].rearrange("p (c i) -> p c i", i=n),
                axis=mybir.AxisListType.X,
                op=ADD,
            )
            pools[n] = const.tile([P, P // n], BF16, name="pool_bf", tag="pool" + str(n))
            nc.vector.tensor_copy(out=pools[n][:], in_=sums_f32[:])

        w_codes = const.tile([P, 4, D_ONE], U32, name="w_codes", align_bytes=64)
        w_scales = const.tile([P, 4, D_ONE], U8, name="w_scales", align_bytes=64)

        w_grouped_tiles = {}

        def group_weights(w_index):
            grouped = []
            for half in range(2):
                w_grouped = w_stage.tile([P, D_ONE, PACK], BF16, name="w_grouped", align_bytes=64)
                copy = nc.vector.tensor_copy if w_index == 0 else nc.scalar.copy
                by_feature = w_raw[w_index][:, PACK * half : PACK * (half + 1), :].rearrange(
                    "p t (u q e) -> p t u q e", u=2, e=2
                )
                for m in range(PACK):
                    u, e = divmod(m, 2)
                    copy(
                        out=w_grouped[:, P * m : P * (m + 1), :].rearrange("p (c i) t -> p c t i", i=4),
                        in_=by_feature[:, :, u, :, e].rearrange("p t (c i) -> p c t i", i=4),
                    )
                grouped.append(w_grouped)
            w_grouped_tiles[w_index] = grouped

        def quantise_weights(w_index):
            grouped = w_grouped_tiles[w_index]
            for half in range(2):
                nc.vector.quantize_mx(
                    out=w_codes[:, 2 * w_index + half, :].bitcast(FP8X4),
                    scales=w_scales[:, 2 * w_index + half, :],
                    in_=grouped[half][:].rearrange("p f t -> p (f t)"),
                )

        h_grouped = []
        g_sums = []
        h_codes = []
        h_scales = []
        g_own = const.tile([P, GROUPS, PACK], BF16, name="g_own", align_bytes=64)
        g_partner = const.tile([P, GROUPS, PACK], BF16, name="g_partner", align_bytes=64)

        def transpose_h(t):
            h_nat = h_tiles[t]
            if t % H_SET == 0:
                h_grouped.append(
                    hset_pool.tile([P, H_SET, P, PACK], BF16, name="h_grouped", align_bytes=64)
                )
            hT = psum_t.tile([P, 2, P], F32, name="hT", tag="hT")
            words = h_nat.bitcast(F32)
            by_parity = h_nat.rearrange("p (u q e) -> p u e q", u=2, e=2)
            for u in range(2):
                nc.tensor.transpose(hT[:, u, :], words[:, P * u : P * (u + 1)], ident_f32[:])
            if t % H_SET == 0:
                g_sums.append(psum_out.tile([P, PACK, H_SET * TILE_GROUPS], F32, name="g_sum", tag="back"))
            for k in range(PACK):
                first = TILE_GROUPS * (t % H_SET)
                nc.tensor.matmul(
                    out=g_sums[-1][:, k, first : first + TILE_GROUPS],
                    lhsT=by_parity[:, k // 2, k % 2, :],
                    rhs=pools[NSPIN][:],
                    start=True,
                    stop=True,
                )
            nc.scalar.copy(
                out=h_grouped[-1][:, t % H_SET, :, :]
                .rearrange("p e k -> p (e k)")
                .bitcast(F32)
                .rearrange("p (e u) -> p e u", u=2),
                in_=hT[:].rearrange("p u e -> p e u"),
            )
            if t % H_SET == H_SET - 1:
                s = t // H_SET
                nc.scalar.mul(
                    out=g_own[:, H_SET * TILE_GROUPS * s : H_SET * TILE_GROUPS * (s + 1), :],
                    in_=g_sums[-1][:].rearrange("p k g -> p g k"),
                    mul=1.0 / NSPIN,
                )

        def quantise_h(s):
            codes = hset_pool.tile([P, H_SET, P], U32, name="h_codes", align_bytes=64)
            scales = hset_pool.tile([P, H_SET, P], U8, name="h_scales", align_bytes=64)
            nc.vector.quantize_mx(
                out=codes[:].rearrange("p c e -> p (c e)").bitcast(FP8X4),
                scales=scales[:].rearrange("p c e -> p (c e)"),
                in_=h_grouped[s][:].rearrange("p c e k -> p (c e k)"),
            )
            h_codes.append(codes)
            h_scales.append(scales)

        g_codes = const.tile([P, 2, GROUPS], U32, name="g_codes", align_bytes=64)
        g_scales = const.tile([P, 2, GROUPS], U8, name="g_scales", align_bytes=64)

        def quantise_groups():
            by_spin = g_own[:].rearrange("p (m s) k -> p m s k", s=2)
            partner_by_spin = g_partner[:].rearrange("p (m s) k -> p m s k", s=2)
            for s in range(2):
                nc.vector.tensor_copy(out=partner_by_spin[:, :, 1 - s, :], in_=by_spin[:, :, s, :])
            for i, g_tile in enumerate((g_own, g_partner)):
                nc.vector.quantize_mx(
                    out=g_codes[:, i, :].bitcast(FP8X4),
                    scales=g_scales[:, i, :],
                    in_=g_tile[:].rearrange("p g k -> p (g k)"),
                )

        b_ps = psum_t.tile([P, 2, P], BF16, name="b_ps", tag="hT")
        by_parity = b_rows[:].rearrange("p (x e) -> p e x", e=2)
        for e in range(2):
            nc.tensor.transpose(b_ps[:, e, :], by_parity[:, e, :], ident_bf[:])
        b_cols = const.tile([P, PACK], F32, name="b_cols")
        nc.scalar.copy(
            out=b_cols[:].rearrange("p (u e) -> p e u", e=2), in_=b_ps[:, :, 0:2]
        )

        cb = const.tile([P, PACK, GROUPS], F32, name="cb")

        def group_product():
            for half in range(2):
                acc = psum_t.tile([P, 2, GROUPS], F32, name="acc_g", tag="hT")
                for i in range(2):
                    m = 2 * half + i
                    for w_pass in range(2):
                        nc.tensor.matmul_mx(
                            out=acc[:, i, :],
                            lhsT=w_codes[:, 2 + w_pass, P * m : P * (m + 1)].bitcast(FP8X4),
                            lhsT_scale=w_scales[:, 2 + w_pass, P * m : P * (m + 1)],
                            rhs=g_codes[:, w_pass, :].bitcast(FP8X4),
                            rhs_scale=g_scales[:, w_pass, :],
                            start=(w_pass == 0),
                            stop=(w_pass == 1),
                        )
                for i in range(2):
                    m = 2 * half + i
                    nc.scalar.activation(
                        out=cb[:, m, :],
                        in_=acc[:, i, :],
                        func=ACT.Identity,
                        bias=b_cols[:, m : m + 1],
                        scale=1.0,
                    )

        def add_rows(t, stream):
            if (t, stream) in MATMUL_UNITS:
                return
            rows = pair_units[t, stream][:].rearrange("p (j f) -> p j f", j=NSPIN)
            sum4 = sums.tile([P, 4, D_TWO], F32, name="sum4", tag=("same4", "diff4")[stream])
            nc.vector.tensor_tensor(out=sum4[:], in0=rows[:, 0:4, :], in1=rows[:, 4:8, :], op=ADD)
            sum_tiles[t, stream] = sum4

        def pool_pairs(t):
            pooled = psum_pair.tile([P, PACK, P], F32, name="pooled")
            pooled_tiles[t] = pooled
            for stream in range(2):
                if (t, stream) in MATMUL_UNITS:
                    chunks = pair_units[t, stream][:].rearrange(
                        "p (c l f) -> p c l f", c=CHUNKS, l=CHUNK_ROWS
                    )
                    for c in range(CHUNKS):
                        for fh in range(2):
                            for l in range(CHUNK_ROWS):
                                nc.tensor.matmul(
                                    out=pooled[:, 2 * stream + fh, CHUNK_COLS * c : CHUNK_COLS * (c + 1)],
                                    lhsT=chunks[:, c, l, P * fh : P * (fh + 1)],
                                    rhs=pools[NSPIN // CHUNK_ROWS][:],
                                    start=(l == 0),
                                    stop=(l == CHUNK_ROWS - 1),
                                )
                else:
                    sum4 = sum_tiles[t, stream]
                    for fh in range(2):
                        for j in range(4):
                            nc.tensor.matmul(
                                out=pooled[:, 2 * stream + fh, :],
                                lhsT=sum4[:, j, P * fh : P * (fh + 1)],
                                rhs=ident_f32[:],
                                start=(j == 0),
                                stop=(j == 3),
                                is_transpose=True,
                            )

        def group_pairs(t):
            grouped = small.tile([P, P, PACK], BF16, name="grouped", align_bytes=64)
            pair_grouped[t] = grouped
            nc.scalar.mul(
                out=grouped[:], in_=pooled_tiles[t][:].rearrange("p k e -> p e k"), mul=1.0 / NSPIN
            )

        def quantise_pairs(t):
            codes = small.tile([P, P], U32, name="codes", align_bytes=64)
            scales = small.tile([P, P], U8, name="scales", align_bytes=64)
            nc.vector.quantize_mx(
                out=codes[:].bitcast(FP8X4),
                scales=scales[:],
                in_=pair_grouped[t][:].rearrange("p e k -> p (e k)"),
            )
            pair_codes[t] = (codes, scales)

        def multiply(t):
            s, i = divmod(t, H_SET)
            moving = (
                (h_codes[s][:, i, :], h_scales[s][:, i, :]),
                (pair_codes[t][0][:], pair_codes[t][1][:]),
            )
            acc = psum_acc.tile([P, PACK, P], F32, name="acc", tag="acc")
            acc_tiles[t] = acc
            for m in range(PACK):
                for w_pass in range(2):
                    nc.tensor.matmul_mx(
                        out=acc[:, m, :],
                        lhsT=w_codes[:, w_pass, P * m : P * (m + 1)].bitcast(FP8X4),
                        lhsT_scale=w_scales[:, w_pass, P * m : P * (m + 1)],
                        rhs=moving[w_pass][0].bitcast(FP8X4),
                        rhs_scale=moving[w_pass][1],
                        start=(w_pass == 0),
                        stop=(w_pass == 1),
                    )

        def add_group_term(t):
            z = small.tile([P, PACK, P], F32, name="z")
            z_tiles[t] = z
            term = cb[:, :, TILE_GROUPS * t : TILE_GROUPS * (t + 1)]
            nc.vector.tensor_tensor(
                out=z[:].rearrange("p m (g i) -> p m g i", i=NSPIN),
                in0=acc_tiles[t][:].rearrange("p m (g i) -> p m g i", i=NSPIN),
                in1=term.unsqueeze(3).to_broadcast([P, PACK, TILE_GROUPS, NSPIN]),
                op=ADD,
            )

        def tanh(t):
            z = z_tiles[t]
            nc.scalar.activation(out=z[:], in_=z[:], func=ACT.Tanh, scale=INV_SQRT2)

        def h_by_feature(t):
            s, i = divmod(t, H_SET)
            return h_grouped[s][:, i, :, :].rearrange("p e k -> p k e")

        def add_residual(t):
            z = z_tiles[t]
            if t in TENSOR_RESIDUAL:
                return
            nc.vector.scalar_tensor_tensor(
                out=z[:], in0=z[:], scalar=TANH_GAIN, in1=h_by_feature(t), op0=MULT, op1=ADD
            )

        def scale_h(t):
            if t not in TENSOR_RESIDUAL:
                return
            hs_tiles[t] = small.tile([P, PACK, P], F32, name="hs")
            nc.scalar.mul(out=hs_tiles[t][:], in_=h_by_feature(t), mul=1.0 / TANH_GAIN)

        def transpose_back(t):
            back = psum_out.tile([P, PACK, P], F32, name="back", tag="back")
            back_tiles[t] = back
            parts = (hs_tiles[t], z_tiles[t]) if t in TENSOR_RESIDUAL else (z_tiles[t],)
            for m in range(PACK):
                for i, part in enumerate(parts):
                    nc.tensor.matmul(
                        out=back[:, m, :],
                        lhsT=part[:, m, :],
                        rhs=ident_f32[:],
                        start=(i == 0),
                        stop=(i == len(parts) - 1),
                        is_transpose=True,
                    )

        def store(t):
            if t % H_SET == 0:
                result_tiles.append(wide.tile([P, H_SET, D_ONE], F32, name="result", tag="wide"))
            i = t % H_SET
            result = result_tiles[-1]
            factor = TANH_GAIN * INV_SQRT2 if t in TENSOR_RESIDUAL else INV_SQRT2
            parts = 2 if t == TILES - 1 else 1
            width = D_ONE // parts
            for part in range(parts):
                columns = slice(width * part, width * (part + 1))
                features = slice(PACK // parts * part, PACK // parts * (part + 1))
                nc.scalar.mul(
                    out=result[:, i, columns].rearrange("p (u q e) -> p u q e", q=P, e=2),
                    in_=back_tiles[t][:, features, :].rearrange("p (u e) q -> p u q e", e=2),
                    mul=factor,
                )
                if parts == 2:
                    nc.sync.dma_start(out=out[P * t : P * (t + 1), columns], in_=result[:, i, columns])
            n = 1 if t >= TILES - 4 else 2
            if parts == 1 and t % n == n - 1:
                first = t - n + 1
                nc.sync.dma_start(
                    out=out[P * first : P * (t + 1), :].rearrange("(q p) f -> p q f", p=P),
                    in_=result[:, i - n + 1 : i + 1, :],
                )

        def is_tile(t):
            return 0 <= t < TILES

        group_weights(0)
        for t in range(TILES):
            transpose_h(t)
        quantise_weights(0)
        for i in range(TILES // H_SET):
            quantise_h(i)
        group_weights(1)
        quantise_groups()
        quantise_weights(1)
        for r in range(TILES + 5):
            if is_tile(r - 4):
                add_group_term(r - 4)
                tanh(r - 4)
            if is_tile(r - 5):
                add_residual(r - 5)
            if is_tile(r):
                add_rows(r, 0)
                add_rows(r, 1)
            if is_tile(r - 2):
                quantise_pairs(r - 2)
            if is_tile(r - 3):
                multiply(r - 3)
                scale_h(r - 3)
            if is_tile(r - 5):
                transpose_back(r - 5)
            if r == 1:
                group_product()
            if is_tile(r - 5):
                store(r - 5)
            if is_tile(r):
                pool_pairs(r)
            if is_tile(r - 1):
                group_pairs(r - 1)
            if r + LOAD_AHEAD < TILES:
                load_pairs(r + LOAD_AHEAD)
